import numpy as np
import ml_dtypes


def mxq(x, axis, fmt="e4m3"):
    dtype, down = {"e4m3": (ml_dtypes.float8_e4m3fn, 7), "e5m2": (ml_dtypes.float8_e5m2, 14)}[fmt]
    v = np.moveaxis(np.asarray(x, np.float32).astype(ml_dtypes.bfloat16).astype(np.float64), axis, -1)
    blocks = v.reshape(v.shape[:-1] + (-1, 32))
    amax = np.abs(blocks).max(-1, keepdims=True)
    byte = np.maximum(np.where(amax > 0, np.frexp(amax)[1] - 1 + 127, 0) - down, 1)
    scale = np.exp2(byte - 127.0)
    codes = (blocks / scale).astype(np.float32).astype(dtype).astype(np.float64)
    return np.moveaxis((codes * scale).reshape(v.shape), -1, axis)


WIDE = False


def mx_kscale(k):
    if not WIDE:
        return np.ones(k)
    levels = np.array([10, -10, 5, -5, 0])
    a = np.random.permutation(np.resize(levels, k // 512 * 4)).reshape(k // 512, 4)
    idx = np.arange(k)
    return np.exp2(a[idx // 512, idx % 128 // 32])


BF16 = ml_dtypes.bfloat16


def bf(x):
    return np.asarray(x, np.float32).astype(BF16)


def f64(x):
    return np.asarray(x).astype(np.float64)


E2M1 = np.array([0.0, 0.5, 1.0, 1.5, 2.0, 3.0, 4.0, 6.0, -0.0, -0.5, -1.0, -1.5, -2.0, -3.0, -4.0, -6.0])


def pack_weight(w, fmt):
    k, n = w.shape
    w = f64(bf(w)).reshape(k // 32, 32, n)
    amax = np.abs(w).max(1)
    if fmt == "e4m3":
        byte = np.frexp(amax)[1] - 1 + 127 - 7
    else:
        mant, ex = np.frexp(amax / 6.0)
        byte = np.where(mant > 0.5, ex, ex - 1) + 127
    byte = np.clip(np.where(amax > 0, byte, 1), 1, 254)
    scaled = (w * np.exp2(127.0 - byte)[:, None, :]).reshape(k, n).astype(np.float32)
    by_word = np.ascontiguousarray(scaled.reshape(k // 512, 128, 4, n).transpose(0, 1, 3, 2))
    if fmt == "e4m3":
        words = by_word.astype(ml_dtypes.float8_e4m3fn).view(np.uint8)
    else:
        c = by_word.astype(ml_dtypes.float4_e2m1fn).view(np.uint8) & 0xF
        words = c[..., 0::2] | (c[..., 1::2] << 4)
    return np.ascontiguousarray(words), np.ascontiguousarray(byte.astype(np.uint8).reshape(k // 512, 16, n))


def unpack_weight(words, scales, fmt):
    g, p, n, _ = words.shape
    if fmt == "e4m3":
        vals = np.ascontiguousarray(words).view(ml_dtypes.float8_e4m3fn).astype(np.float64)
    else:
        nib = np.empty((g, p, n, 4), np.uint8)
        nib[..., 0::2] = words & 0xF
        nib[..., 1::2] = words >> 4
        vals = E2M1[nib]
    vals = vals * np.repeat(np.exp2(scales.astype(np.float64) - 127.0), 8, axis=1)[..., None]
    return vals.transpose(0, 1, 3, 2).reshape(g * 512, n)


B, S, K, N = 2, 512, 2048, 2048
FMT = "e4m3"


def setup_inputs():
    s = mx_kscale(K)
    input = bf(np.random.standard_normal((B, S, K)) * s)
    weight = np.random.standard_normal((N, K)) / np.sqrt(K) / s[None, :]
    words, scales = pack_weight(np.ascontiguousarray(weight.T), FMT)
    bias = bf(np.random.standard_normal(N) * 0.5)
    return {"input": input,
            "weight_words": words,
            "weight_scales": scales,
            "bias": bias}


def reference(input, weight_words, weight_scales, bias):
    xq = mxq(f64(input), 2, "e4m3")
    wq = unpack_weight(weight_words, weight_scales, FMT)
    out = xq.reshape(B * S, K) @ wq
    return out.reshape(B, S, N) + f64(bias)

@@ -1,0 +1,163 @@
+from contextlib import ExitStack
+
+import concourse.mybir as mybir
+from concourse.masks import make_identity
+
+F32 = mybir.dt.float32
+BF16 = mybir.dt.bfloat16
+I32 = mybir.dt.int32
+U32 = mybir.dt.uint32
+U8 = mybir.dt.uint8
+FP8X4 = mybir.dt.float8_e4m3fn_x4
+
+P = 128
+PACK = 4
+K_PASS = P * PACK
+TOKENS = 1024
+K = 2048
+N = 2048
+PASSES = K // K_PASS
+TOKEN_TILES = TOKENS // P
+PAIR = 2
+PAIRS = TOKEN_TILES // PAIR
+BANK = 512
+HALF = N // 2
+HALVES = N // HALF
+BANKS_PER_HALF = HALF // BANK
+WORDS_PER_PASS = K_PASS // 2
+
+FLOPS = 2 * TOKENS * K * N
+
+
+def tile_tiledlinear_kernel(tc, x, weight_words, weight_scales, bias, out):
+    nc = tc.nc
+    x_rows = x.flatten_outer_dims()
+    out_rows = out.flatten_outer_dims()
+
+    with ExitStack() as ctx:
+        keep = ctx.enter_context(tc.tile_pool(name="keep", bufs=1))
+        stage = ctx.enter_context(tc.tile_pool(name="stage", bufs=2))
+        results = ctx.enter_context(tc.tile_pool(name="results", bufs=TOKEN_TILES * HALVES))
+        psum = ctx.enter_context(tc.psum_pool(name="psum", bufs=8))
+
+        x_raw = [keep.tile([P, K], BF16, name="x_raw%d" % m) for m in range(TOKEN_TILES)]
+        x_codes = [
+            keep.tile([P, PASSES * P], U32, name="x_codes%d" % m, align_bytes=64) for m in range(TOKEN_TILES)
+        ]
+        x_planes = [
+            keep.tile([P, PASSES * P], U8, name="x_planes%d" % m, align_bytes=64) for m in range(TOKEN_TILES)
+        ]
+        w_codes = [
+            [keep.tile([P, HALF], U32, name="w_codes%d_%d" % (g, h), align_bytes=64) for h in range(HALVES)]
+            for g in range(PASSES)
+        ]
+        w_planes = keep.tile([P, N], U8, name="w_planes", align_bytes=64)
+        bias_rows = keep.tile([P, N], BF16, name="bias_rows")
+        bias_all = keep.tile([P, N], F32, name="bias_all")
+        ones = keep.tile([P, P], BF16, name="ones")
+        ident = keep.tile([P, P], F32, name="ident")
+
+        nc.vector.memset(w_planes[:].bitcast(I32), 0)
+        nc.vector.memset(bias_rows[:], 0.0)
+        nc.vector.memset(ones[:], 1.0)
+        make_identity(nc, ident[:])
+        nc.scalar.dma_start(out=bias_rows[0:1, :], in_=bias.rearrange("(o n) -> o n", o=1))
+
+        def load_x(m):
+            nc.sync.dma_start(out=x_raw[m][:], in_=x_rows[m * P : (m + 1) * P, :])
+
+        def load_w_planes():
+            for quadrant in range(4):
+                nc.sync.dma_start(
+                    out=w_planes[32 * quadrant : 32 * quadrant + 16, :].bitcast(I32),
+                    in_=weight_scales[:, 4 * quadrant : 4 * quadrant + 4, :].bitcast(I32),
+                )
+
+        def load_w_half(h):
+            for g in range(PASSES):
+                w_bytes = weight_words[g].rearrange("p n t -> p (n t)")
+                nc.sync.dma_start(
+                    out=w_codes[g][h][:].bitcast(I32),
+                    in_=w_bytes[:, PACK * HALF * h : PACK * HALF * (h + 1)].bitcast(I32),
+                )
+
+        load_x(0)
+        load_x(1)
+        load_w_planes()
+        load_w_half(0)
+        load_x(2)
+        load_x(3)
+        load_w_half(1)
+        for m in range(4, TOKEN_TILES):
+            load_x(m)
+
+        def quantise_pair(q):
+            grouped = stage.tile([P, PAIR, PASSES, P, PACK], BF16, name="grouped", align_bytes=64)
+            for i in range(PAIR):
+                m = PAIR * q + i
+                x_words = x_raw[m][:].bitcast(F32)
+                for first_pass in range(0, PASSES, 2):
+                    turned = psum.tile([P, 2, 2, P], F32, name="turned", tag="bank")
+                    for j in range(2):
+                        g = first_pass + j
+                        for u in range(2):
+                            nc.tensor.transpose(
+                                turned[:, j, u, :],
+                                x_words[:, WORDS_PER_PASS * g + u : WORDS_PER_PASS * (g + 1) : 2],
+                                ident[:],
+                            )
+                    nc.scalar.copy(
+                        out=grouped[:, i, first_pass : first_pass + 2, :, :].bitcast(F32),
+                        in_=turned[:].rearrange("p j u t -> p j t u"),
+                    )
+                nc.vector.quantize_mx(
+                    out=x_codes[m][:].bitcast(FP8X4),
+                    scales=x_planes[m][:],
+                    in_=grouped[:, i].rearrange("p g t j -> p (g t j)"),
+                )
+
+        def spread_bias():
+            for c in range(N // BANK):
+                cols = slice(c * BANK, (c + 1) * BANK)
+                spread = psum.tile([P, BANK], F32, name="spread", tag="bank")
+                nc.tensor.matmul(spread[:], lhsT=ones[:], rhs=bias_rows[:, cols], start=True, stop=True)
+                nc.scalar.copy(out=bias_all[:, cols], in_=spread[:])
+
+        def multiply_block(q, h):
+            acc = {}
+            for i in range(PAIR):
+                for c in range(BANKS_PER_HALF):
+                    acc[i, c] = psum.tile([P, BANK], F32, name="acc%d%d" % (i, c), tag="bank")
+            for g in range(PASSES):
+                for i in range(PAIR):
+                    m = PAIR * q + i
+                    for c in range(BANKS_PER_HALF):
+                        nc.tensor.matmul_mx(
+                            out=acc[i, c][:],
+                            lhsT=x_codes[m][:, g * P : (g + 1) * P].bitcast(FP8X4),
+                            lhsT_scale=x_planes[m][:, g * P : (g + 1) * P],
+                            rhs=w_codes[g][h][:, c * BANK : (c + 1) * BANK].bitcast(FP8X4),
+                            rhs_scale=w_planes[4 * g : P, h * HALF + c * BANK : h * HALF + (c + 1) * BANK],
+                            start=(g == 0),
+                            stop=(g == PASSES - 1),
+                        )
+            for i in range(PAIR):
+                m = PAIR * q + i
+                result = results.tile([P, HALF], F32, name="result")
+                for c in range(BANKS_PER_HALF):
+                    nc.vector.tensor_tensor(
+                        out=result[:, c * BANK : (c + 1) * BANK],
+                        in0=acc[i, c][:],
+                        in1=bias_all[:, h * HALF + c * BANK : h * HALF + (c + 1) * BANK],
+                        op=mybir.AluOpType.add,
+                    )
+                nc.sync.dma_start(out=out_rows[m * P : (m + 1) * P, h * HALF : (h + 1) * HALF], in_=result[:])
+
+        quantise_pair(0)
+        spread_bias()
+        multiply_block(0, 0)
+        for q in range(1, PAIRS):
+            quantise_pair(q)
+            multiply_block(q - 1, 1)
+            multiply_block(q, 0)
+        multiply_block(PAIRS - 1, 1)

@@ -24,7 +24,6 @@ BANK = 512
 HALF = N // 2
 HALVES = N // HALF
 BANKS_PER_HALF = HALF // BANK
-WORDS_PER_PASS = K_PASS // 2
 
 FLOPS = 2 * TOKENS * K * N
 
@@ -95,17 +94,17 @@ def tile_tiledlinear_kernel(tc, x, weight_words, weight_scales, bias, out):
             grouped = stage.tile([P, PAIR, PASSES, P, PACK], BF16, name="grouped", align_bytes=64)
             for i in range(PAIR):
                 m = PAIR * q + i
-                x_words = x_raw[m][:].bitcast(F32)
+                x_sorted = stage.tile([P, PASSES, 2, P], F32, name="x_sorted")
+                nc.vector.tensor_copy(
+                    out=x_sorted[:],
+                    in_=x_raw[m][:].bitcast(F32).rearrange("t (g p u) -> t g u p", g=PASSES, u=2),
+                )
                 for first_pass in range(0, PASSES, 2):
                     turned = psum.tile([P, 2, 2, P], F32, name="turned", tag="bank")
                     for j in range(2):
                         g = first_pass + j
                         for u in range(2):
-                            nc.tensor.transpose(
-                                turned[:, j, u, :],
-                                x_words[:, WORDS_PER_PASS * g + u : WORDS_PER_PASS * (g + 1) : 2],
-                                ident[:],
-                            )
+                            nc.tensor.transpose(turned[:, j, u, :], x_sorted[:, g, u, :], ident[:])
                     nc.scalar.copy(
                         out=grouped[:, i, first_pass : first_pass + 2, :, :].bitcast(F32),
                         in_=turned[:].rearrange("p j u t -> p j t u"),

@@ -36,8 +36,9 @@ def tile_tiledlinear_kernel(tc, x, weight_words, weight_scales, bias, out):
     with ExitStack() as ctx:
         keep = ctx.enter_context(tc.tile_pool(name="keep", bufs=1))
         stage = ctx.enter_context(tc.tile_pool(name="stage", bufs=2))
-        results = ctx.enter_context(tc.tile_pool(name="results", bufs=TOKEN_TILES * HALVES))
+        results = ctx.enter_context(tc.tile_pool(name="results", bufs=TOKEN_TILES * (N // BANK)))
         psum = ctx.enter_context(tc.psum_pool(name="psum", bufs=8))
+        ctx.enter_context(tc.manual_schedule())
 
         x_raw = [keep.tile([P, K], BF16, name="x_raw%d" % m) for m in range(TOKEN_TILES)]
         x_codes = [
@@ -90,21 +91,26 @@ def tile_tiledlinear_kernel(tc, x, weight_words, weight_scales, bias, out):
         for m in range(4, TOKEN_TILES):
             load_x(m)
 
+        x_sorted = {}
+
+        def sort_pair(q):
+            for m in range(PAIR * q, PAIR * (q + 1)):
+                x_sorted[m] = stage.tile([P, PASSES, 2, P], F32, name="x_sorted")
+                nc.vector.tensor_copy(
+                    out=x_sorted[m][:],
+                    in_=x_raw[m][:].bitcast(F32).rearrange("t (g p u) -> t g u p", g=PASSES, u=2),
+                )
+
         def quantise_pair(q):
             grouped = stage.tile([P, PAIR, PASSES, P, PACK], BF16, name="grouped", align_bytes=64)
             for i in range(PAIR):
                 m = PAIR * q + i
-                x_sorted = stage.tile([P, PASSES, 2, P], F32, name="x_sorted")
-                nc.vector.tensor_copy(
-                    out=x_sorted[:],
-                    in_=x_raw[m][:].bitcast(F32).rearrange("t (g p u) -> t g u p", g=PASSES, u=2),
-                )
                 for first_pass in range(0, PASSES, 2):
                     turned = psum.tile([P, 2, 2, P], F32, name="turned", tag="bank")
                     for j in range(2):
                         g = first_pass + j
                         for u in range(2):
-                            nc.tensor.transpose(turned[:, j, u, :], x_sorted[:, g, u, :], ident[:])
+                            nc.tensor.transpose(turned[:, j, u, :], x_sorted[m][:, g, u, :], ident[:])
                     nc.scalar.copy(
                         out=grouped[:, i, first_pass : first_pass + 2, :, :].bitcast(F32),
                         in_=turned[:].rearrange("p j u t -> p j t u"),
@@ -123,40 +129,41 @@ def tile_tiledlinear_kernel(tc, x, weight_words, weight_scales, bias, out):
                 nc.scalar.copy(out=bias_all[:, cols], in_=spread[:])
 
         def multiply_block(q, h):
+            groups = [(i, c) for i in range(PAIR) for c in range(BANKS_PER_HALF)]
+            if q == 0:
+                order = [(g, i, c) for g in range(PASSES) for (i, c) in groups]
+            else:
+                order = [(g, i, c) for (i, c) in groups for g in range(PASSES)]
             acc = {}
-            for i in range(PAIR):
-                for c in range(BANKS_PER_HALF):
-                    acc[i, c] = psum.tile([P, BANK], F32, name="acc%d%d" % (i, c), tag="bank")
-            for g in range(PASSES):
-                for i in range(PAIR):
-                    m = PAIR * q + i
-                    for c in range(BANKS_PER_HALF):
-                        nc.tensor.matmul_mx(
-                            out=acc[i, c][:],
-                            lhsT=x_codes[m][:, g * P : (g + 1) * P].bitcast(FP8X4),
-                            lhsT_scale=x_planes[m][:, g * P : (g + 1) * P],
-                            rhs=w_codes[g][h][:, c * BANK : (c + 1) * BANK].bitcast(FP8X4),
-                            rhs_scale=w_planes[4 * g : P, h * HALF + c * BANK : h * HALF + (c + 1) * BANK],
-                            start=(g == 0),
-                            stop=(g == PASSES - 1),
-                        )
-            for i in range(PAIR):
+            for i, c in groups:
+                acc[i, c] = psum.tile([P, BANK], F32, name="acc%d%d" % (i, c), tag="bank")
+            for g, i, c in order:
                 m = PAIR * q + i
-                result = results.tile([P, HALF], F32, name="result")
-                for c in range(BANKS_PER_HALF):
-                    nc.vector.tensor_tensor(
-                        out=result[:, c * BANK : (c + 1) * BANK],
-                        in0=acc[i, c][:],
-                        in1=bias_all[:, h * HALF + c * BANK : h * HALF + (c + 1) * BANK],
-                        op=mybir.AluOpType.add,
-                    )
-                nc.sync.dma_start(out=out_rows[m * P : (m + 1) * P, h * HALF : (h + 1) * HALF], in_=result[:])
+                nc.tensor.matmul_mx(
+                    out=acc[i, c][:],
+                    lhsT=x_codes[m][:, g * P : (g + 1) * P].bitcast(FP8X4),
+                    lhsT_scale=x_planes[m][:, g * P : (g + 1) * P],
+                    rhs=w_codes[g][h][:, c * BANK : (c + 1) * BANK].bitcast(FP8X4),
+                    rhs_scale=w_planes[4 * g : P, h * HALF + c * BANK : h * HALF + (c + 1) * BANK],
+                    start=(g == 0),
+                    stop=(g == PASSES - 1),
+                )
+            for i, c in groups:
+                m = PAIR * q + i
+                n_cols = slice(h * HALF + c * BANK, h * HALF + (c + 1) * BANK)
+                result = results.tile([P, BANK], F32, name="result")
+                nc.vector.tensor_tensor(out=result[:], in0=acc[i, c][:], in1=bias_all[:, n_cols], op=mybir.AluOpType.add)
+                nc.sync.dma_start(out=out_rows[m * P : (m + 1) * P, n_cols], in_=result[:])
 
+        sort_pair(0)
         quantise_pair(0)
         spread_bias()
+        sort_pair(1)
         multiply_block(0, 0)
         for q in range(1, PAIRS):
             quantise_pair(q)
             multiply_block(q - 1, 1)
+            if q + 1 < PAIRS:
+                sort_pair(q + 1)
             multiply_block(q, 0)
         multiply_block(PAIRS - 1, 1)

@@ -23,7 +23,11 @@ PAIRS = TOKEN_TILES // PAIR
 BANK = 512
 HALF = N // 2
 HALVES = N // HALF
-BANKS_PER_HALF = HALF // BANK
+SLAB_PASSES = 2
+SLABS = PASSES // SLAB_PASSES
+K_SLAB = SLAB_PASSES * K_PASS
+LAST_WIDTH = BANK // 2
+RESULT_TILES = (PAIRS * HALVES - 1) * PAIR * (HALF // BANK) + PAIR * (HALF // LAST_WIDTH)
 
 FLOPS = 2 * TOKENS * K * N
 
@@ -35,17 +39,19 @@ def tile_tiledlinear_kernel(tc, x, weight_words, weight_scales, bias, out):
 
     with ExitStack() as ctx:
         keep = ctx.enter_context(tc.tile_pool(name="keep", bufs=1))
-        stage = ctx.enter_context(tc.tile_pool(name="stage", bufs=2))
-        results = ctx.enter_context(tc.tile_pool(name="results", bufs=TOKEN_TILES * (N // BANK)))
+        stage = ctx.enter_context(tc.tile_pool(name="stage", bufs=PAIR * SLABS))
+        results = ctx.enter_context(tc.tile_pool(name="results", bufs=RESULT_TILES))
         psum = ctx.enter_context(tc.psum_pool(name="psum", bufs=8))
         ctx.enter_context(tc.manual_schedule())
 
         x_raw = [keep.tile([P, K], BF16, name="x_raw%d" % m) for m in range(TOKEN_TILES)]
         x_codes = [
-            keep.tile([P, PASSES * P], U32, name="x_codes%d" % m, align_bytes=64) for m in range(TOKEN_TILES)
+            [keep.tile([P, SLAB_PASSES * P], U32, name="x_codes%d_%d" % (m, s), align_bytes=64) for s in range(SLABS)]
+            for m in range(TOKEN_TILES)
         ]
         x_planes = [
-            keep.tile([P, PASSES * P], U8, name="x_planes%d" % m, align_bytes=64) for m in range(TOKEN_TILES)
+            [keep.tile([P, SLAB_PASSES * P], U8, name="x_planes%d_%d" % (m, s), align_bytes=64) for s in range(SLABS)]
+            for m in range(TOKEN_TILES)
         ]
         w_codes = [
             [keep.tile([P, HALF], U32, name="w_codes%d_%d" % (g, h), align_bytes=64) for h in range(HALVES)]
@@ -57,11 +63,11 @@ def tile_tiledlinear_kernel(tc, x, weight_words, weight_scales, bias, out):
         ones = keep.tile([P, P], BF16, name="ones")
         ident = keep.tile([P, P], F32, name="ident")
 
-        nc.vector.memset(w_planes[:].bitcast(I32), 0)
-        nc.vector.memset(bias_rows[:], 0.0)
-        nc.vector.memset(ones[:], 1.0)
-        make_identity(nc, ident[:])
+        nc.vector.memset(bias_rows[:].bitcast(I32), 0)
         nc.scalar.dma_start(out=bias_rows[0:1, :], in_=bias.rearrange("(o n) -> o n", o=1))
+        nc.vector.memset(ones[:], 1.0)
+        nc.vector.memset(w_planes[:].bitcast(I32), 0)
+        make_identity(nc, ident[:])
 
         def load_x(m):
             nc.sync.dma_start(out=x_raw[m][:], in_=x_rows[m * P : (m + 1) * P, :])
@@ -91,36 +97,6 @@ def tile_tiledlinear_kernel(tc, x, weight_words, weight_scales, bias, out):
         for m in range(4, TOKEN_TILES):
             load_x(m)
 
-        x_sorted = {}
-
-        def sort_pair(q):
-            for m in range(PAIR * q, PAIR * (q + 1)):
-                x_sorted[m] = stage.tile([P, PASSES, 2, P], F32, name="x_sorted")
-                nc.vector.tensor_copy(
-                    out=x_sorted[m][:],
-                    in_=x_raw[m][:].bitcast(F32).rearrange("t (g p u) -> t g u p", g=PASSES, u=2),
-                )
-
-        def quantise_pair(q):
-            grouped = stage.tile([P, PAIR, PASSES, P, PACK], BF16, name="grouped", align_bytes=64)
-            for i in range(PAIR):
-                m = PAIR * q + i
-                for first_pass in range(0, PASSES, 2):
-                    turned = psum.tile([P, 2, 2, P], F32, name="turned", tag="bank")
-                    for j in range(2):
-                        g = first_pass + j
-                        for u in range(2):
-                            nc.tensor.transpose(turned[:, j, u, :], x_sorted[m][:, g, u, :], ident[:])
-                    nc.scalar.copy(
-                        out=grouped[:, i, first_pass : first_pass + 2, :, :].bitcast(F32),
-                        in_=turned[:].rearrange("p j u t -> p j t u"),
-                    )
-                nc.vector.quantize_mx(
-                    out=x_codes[m][:].bitcast(FP8X4),
-                    scales=x_planes[m][:],
-                    in_=grouped[:, i].rearrange("p g t j -> p (g t j)"),
-                )
-
         def spread_bias():
             for c in range(N // BANK):
                 cols = slice(c * BANK, (c + 1) * BANK)
@@ -128,30 +104,61 @@ def tile_tiledlinear_kernel(tc, x, weight_words, weight_scales, bias, out):
                 nc.tensor.matmul(spread[:], lhsT=ones[:], rhs=bias_rows[:, cols], start=True, stop=True)
                 nc.scalar.copy(out=bias_all[:, cols], in_=spread[:])
 
+        x_sorted = {}
+
+        def sort_pair(q):
+            for m in range(PAIR * q, PAIR * (q + 1)):
+                for s in range(SLABS):
+                    x_sorted[m, s] = stage.tile([P, SLAB_PASSES, 2, P], F32, name="x_sorted")
+                    nc.vector.tensor_copy(
+                        out=x_sorted[m, s][:],
+                        in_=x_raw[m][:, K_SLAB * s : K_SLAB * (s + 1)]
+                        .bitcast(F32)
+                        .rearrange("t (j p u) -> t j u p", j=SLAB_PASSES, u=2),
+                    )
+
+        def quantise_pair(q):
+            for m in range(PAIR * q, PAIR * (q + 1)):
+                for s in range(SLABS):
+                    turned = psum.tile([P, SLAB_PASSES, 2, P], F32, name="turned", tag="bank")
+                    for j in range(SLAB_PASSES):
+                        for u in range(2):
+                            nc.tensor.transpose(turned[:, j, u, :], x_sorted[m, s][:, j, u, :], ident[:])
+                    grouped = stage.tile([P, SLAB_PASSES, P, PACK], BF16, name="grouped", align_bytes=64)
+                    nc.scalar.copy(out=grouped[:].bitcast(F32), in_=turned[:].rearrange("p j u t -> p j t u"))
+                    nc.vector.quantize_mx(
+                        out=x_codes[m][s][:].bitcast(FP8X4),
+                        scales=x_planes[m][s][:],
+                        in_=grouped[:].rearrange("p j t e -> p (j t e)"),
+                    )
+
         def multiply_block(q, h):
-            groups = [(i, c) for i in range(PAIR) for c in range(BANKS_PER_HALF)]
+            last_block = q == PAIRS - 1 and h == HALVES - 1
+            width = LAST_WIDTH if last_block else BANK
+            groups = [(i, c) for i in range(PAIR) for c in range(HALF // width)]
             if q == 0:
                 order = [(g, i, c) for g in range(PASSES) for (i, c) in groups]
             else:
                 order = [(g, i, c) for (i, c) in groups for g in range(PASSES)]
             acc = {}
             for i, c in groups:
-                acc[i, c] = psum.tile([P, BANK], F32, name="acc%d%d" % (i, c), tag="bank")
+                acc[i, c] = psum.tile([P, width], F32, name="acc%d%d" % (i, c), tag="bank")
             for g, i, c in order:
+                s, j = divmod(g, SLAB_PASSES)
                 m = PAIR * q + i
                 nc.tensor.matmul_mx(
                     out=acc[i, c][:],
-                    lhsT=x_codes[m][:, g * P : (g + 1) * P].bitcast(FP8X4),
-                    lhsT_scale=x_planes[m][:, g * P : (g + 1) * P],
-                    rhs=w_codes[g][h][:, c * BANK : (c + 1) * BANK].bitcast(FP8X4),
-                    rhs_scale=w_planes[4 * g : P, h * HALF + c * BANK : h * HALF + (c + 1) * BANK],
+                    lhsT=x_codes[m][s][:, j * P : (j + 1) * P].bitcast(FP8X4),
+                    lhsT_scale=x_planes[m][s][:, j * P : (j + 1) * P],
+                    rhs=w_codes[g][h][:, c * width : (c + 1) * width].bitcast(FP8X4),
+                    rhs_scale=w_planes[4 * g : P, h * HALF + c * width : h * HALF + (c + 1) * width],
                     start=(g == 0),
                     stop=(g == PASSES - 1),
                 )
             for i, c in groups:
                 m = PAIR * q + i
-                n_cols = slice(h * HALF + c * BANK, h * HALF + (c + 1) * BANK)
-                result = results.tile([P, BANK], F32, name="result")
+                n_cols = slice(h * HALF + c * width, h * HALF + (c + 1) * width)
+                result = results.tile([P, width], F32, name="result")
                 nc.vector.tensor_tensor(out=result[:], in0=acc[i, c][:], in1=bias_all[:, n_cols], op=mybir.AluOpType.add)
                 nc.sync.dma_start(out=out_rows[m * P : (m + 1) * P, n_cols], in_=result[:])
 

@@ -23,11 +23,7 @@ PAIRS = TOKEN_TILES // PAIR
 BANK = 512
 HALF = N // 2
 HALVES = N // HALF
-SLAB_PASSES = 2
-SLABS = PASSES // SLAB_PASSES
-K_SLAB = SLAB_PASSES * K_PASS
-LAST_WIDTH = BANK // 2
-RESULT_TILES = (PAIRS * HALVES - 1) * PAIR * (HALF // BANK) + PAIR * (HALF // LAST_WIDTH)
+BANKS_PER_HALF = HALF // BANK
 
 FLOPS = 2 * TOKENS * K * N
 
@@ -39,19 +35,17 @@ def tile_tiledlinear_kernel(tc, x, weight_words, weight_scales, bias, out):
 
     with ExitStack() as ctx:
         keep = ctx.enter_context(tc.tile_pool(name="keep", bufs=1))
-        stage = ctx.enter_context(tc.tile_pool(name="stage", bufs=PAIR * SLABS))
-        results = ctx.enter_context(tc.tile_pool(name="results", bufs=RESULT_TILES))
+        stage = ctx.enter_context(tc.tile_pool(name="stage", bufs=2))
+        results = ctx.enter_context(tc.tile_pool(name="results", bufs=TOKEN_TILES * (N // BANK)))
         psum = ctx.enter_context(tc.psum_pool(name="psum", bufs=8))
         ctx.enter_context(tc.manual_schedule())
 
         x_raw = [keep.tile([P, K], BF16, name="x_raw%d" % m) for m in range(TOKEN_TILES)]
         x_codes = [
-            [keep.tile([P, SLAB_PASSES * P], U32, name="x_codes%d_%d" % (m, s), align_bytes=64) for s in range(SLABS)]
-            for m in range(TOKEN_TILES)
+            keep.tile([P, PASSES * P], U32, name="x_codes%d" % m, align_bytes=64) for m in range(TOKEN_TILES)
         ]
         x_planes = [
-            [keep.tile([P, SLAB_PASSES * P], U8, name="x_planes%d_%d" % (m, s), align_bytes=64) for s in range(SLABS)]
-            for m in range(TOKEN_TILES)
+            keep.tile([P, PASSES * P], U8, name="x_planes%d" % m, align_bytes=64) for m in range(TOKEN_TILES)
         ]
         w_codes = [
             [keep.tile([P, HALF], U32, name="w_codes%d_%d" % (g, h), align_bytes=64) for h in range(HALVES)]
@@ -63,11 +57,11 @@ def tile_tiledlinear_kernel(tc, x, weight_words, weight_scales, bias, out):
         ones = keep.tile([P, P], BF16, name="ones")
         ident = keep.tile([P, P], F32, name="ident")
 
-        nc.vector.memset(bias_rows[:].bitcast(I32), 0)
-        nc.scalar.dma_start(out=bias_rows[0:1, :], in_=bias.rearrange("(o n) -> o n", o=1))
-        nc.vector.memset(ones[:], 1.0)
         nc.vector.memset(w_planes[:].bitcast(I32), 0)
+        nc.vector.memset(bias_rows[:], 0.0)
+        nc.vector.memset(ones[:], 1.0)
         make_identity(nc, ident[:])
+        nc.scalar.dma_start(out=bias_rows[0:1, :], in_=bias.rearrange("(o n) -> o n", o=1))
 
         def load_x(m):
             nc.sync.dma_start(out=x_raw[m][:], in_=x_rows[m * P : (m + 1) * P, :])
@@ -87,15 +81,40 @@ def tile_tiledlinear_kernel(tc, x, weight_words, weight_scales, bias, out):
                     in_=w_bytes[:, PACK * HALF * h : PACK * HALF * (h + 1)].bitcast(I32),
                 )
 
-        load_x(0)
-        load_x(1)
+        for m in range(2 * PAIR):
+            load_x(m)
         load_w_planes()
         load_w_half(0)
-        load_x(2)
-        load_x(3)
         load_w_half(1)
-        for m in range(4, TOKEN_TILES):
+        for m in range(2 * PAIR, TOKEN_TILES):
             load_x(m)
+
+        x_sorted = {}
+
+        def sort_tile(m):
+            x_sorted[m] = stage.tile([P, PASSES, 2, P], F32, name="x_sorted")
+            nc.vector.tensor_copy(
+                out=x_sorted[m][:],
+                in_=x_raw[m][:].bitcast(F32).rearrange("t (g p u) -> t g u p", g=PASSES, u=2),
+            )
+
+        def quantise_tile(m):
+            grouped = stage.tile([P, PASSES, P, PACK], BF16, name="grouped", align_bytes=64)
+            for first_pass in range(0, PASSES, 2):
+                turned = psum.tile([P, 2, 2, P], F32, name="turned", tag="bank")
+                for j in range(2):
+                    g = first_pass + j
+                    for u in range(2):
+                        nc.tensor.transpose(turned[:, j, u, :], x_sorted[m][:, g, u, :], ident[:])
+                nc.scalar.copy(
+                    out=grouped[:, first_pass : first_pass + 2, :, :].bitcast(F32),
+                    in_=turned[:].rearrange("p j u t -> p j t u"),
+                )
+            nc.vector.quantize_mx(
+                out=x_codes[m][:].bitcast(FP8X4),
+                scales=x_planes[m][:],
+                in_=grouped[:].rearrange("p g t j -> p (g t j)"),
+            )
 
         def spread_bias():
             for c in range(N // BANK):
@@ -104,73 +123,55 @@ def tile_tiledlinear_kernel(tc, x, weight_words, weight_scales, bias, out):
                 nc.tensor.matmul(spread[:], lhsT=ones[:], rhs=bias_rows[:, cols], start=True, stop=True)
                 nc.scalar.copy(out=bias_all[:, cols], in_=spread[:])
 
-        x_sorted = {}
-
-        def sort_pair(q):
-            for m in range(PAIR * q, PAIR * (q + 1)):
-                for s in range(SLABS):
-                    x_sorted[m, s] = stage.tile([P, SLAB_PASSES, 2, P], F32, name="x_sorted")
-                    nc.vector.tensor_copy(
-                        out=x_sorted[m, s][:],
-                        in_=x_raw[m][:, K_SLAB * s : K_SLAB * (s + 1)]
-                        .bitcast(F32)
-                        .rearrange("t (j p u) -> t j u p", j=SLAB_PASSES, u=2),
-                    )
-
-        def quantise_pair(q):
-            for m in range(PAIR * q, PAIR * (q + 1)):
-                for s in range(SLABS):
-                    turned = psum.tile([P, SLAB_PASSES, 2, P], F32, name="turned", tag="bank")
-                    for j in range(SLAB_PASSES):
-                        for u in range(2):
-                            nc.tensor.transpose(turned[:, j, u, :], x_sorted[m, s][:, j, u, :], ident[:])
-                    grouped = stage.tile([P, SLAB_PASSES, P, PACK], BF16, name="grouped", align_bytes=64)
-                    nc.scalar.copy(out=grouped[:].bitcast(F32), in_=turned[:].rearrange("p j u t -> p j t u"))
-                    nc.vector.quantize_mx(
-                        out=x_codes[m][s][:].bitcast(FP8X4),
-                        scales=x_planes[m][s][:],
-                        in_=grouped[:].rearrange("p j t e -> p (j t e)"),
-                    )
-
         def multiply_block(q, h):
-            last_block = q == PAIRS - 1 and h == HALVES - 1
-            width = LAST_WIDTH if last_block else BANK
-            groups = [(i, c) for i in range(PAIR) for c in range(HALF // width)]
+            groups = [(i, c) for i in range(PAIR) for c in range(BANKS_PER_HALF)]
             if q == 0:
                 order = [(g, i, c) for g in range(PASSES) for (i, c) in groups]
             else:
                 order = [(g, i, c) for (i, c) in groups for g in range(PASSES)]
             acc = {}
             for i, c in groups:
-                acc[i, c] = psum.tile([P, width], F32, name="acc%d%d" % (i, c), tag="bank")
+                acc[i, c] = psum.tile([P, BANK], F32, name="acc%d%d" % (i, c), tag="bank")
             for g, i, c in order:
-                s, j = divmod(g, SLAB_PASSES)
                 m = PAIR * q + i
                 nc.tensor.matmul_mx(
                     out=acc[i, c][:],
-                    lhsT=x_codes[m][s][:, j * P : (j + 1) * P].bitcast(FP8X4),
-                    lhsT_scale=x_planes[m][s][:, j * P : (j + 1) * P],
-                    rhs=w_codes[g][h][:, c * width : (c + 1) * width].bitcast(FP8X4),
-                    rhs_scale=w_planes[4 * g : P, h * HALF + c * width : h * HALF + (c + 1) * width],
+                    lhsT=x_codes[m][:, g * P : (g + 1) * P].bitcast(FP8X4),
+                    lhsT_scale=x_planes[m][:, g * P : (g + 1) * P],
+                    rhs=w_codes[g][h][:, c * BANK : (c + 1) * BANK].bitcast(FP8X4),
+                    rhs_scale=w_planes[4 * g : P, h * HALF + c * BANK : h * HALF + (c + 1) * BANK],
                     start=(g == 0),
                     stop=(g == PASSES - 1),
                 )
             for i, c in groups:
                 m = PAIR * q + i
-                n_cols = slice(h * HALF + c * width, h * HALF + (c + 1) * width)
-                result = results.tile([P, width], F32, name="result")
+                n_cols = slice(h * HALF + c * BANK, h * HALF + (c + 1) * BANK)
+                result = results.tile([P, BANK], F32, name="result")
                 nc.vector.tensor_tensor(out=result[:], in0=acc[i, c][:], in1=bias_all[:, n_cols], op=mybir.AluOpType.add)
                 nc.sync.dma_start(out=out_rows[m * P : (m + 1) * P, n_cols], in_=result[:])
 
-        sort_pair(0)
-        quantise_pair(0)
+        sort_tile(0)
+        sort_tile(1)
+        quantise_tile(0)
+        sort_tile(2)
+        quantise_tile(1)
         spread_bias()
-        sort_pair(1)
+        sort_tile(3)
+        quantise_tile(2)
+        quantise_tile(3)
         multiply_block(0, 0)
-        for q in range(1, PAIRS):
-            quantise_pair(q)
-            multiply_block(q - 1, 1)
-            if q + 1 < PAIRS:
-                sort_pair(q + 1)
-            multiply_block(q, 0)
-        multiply_block(PAIRS - 1, 1)
+        multiply_block(1, 0)
+        sort_tile(4)
+        sort_tile(5)
+        multiply_block(0, 1)
+        quantise_tile(4)
+        quantise_tile(5)
+        multiply_block(1, 1)
+        sort_tile(6)
+        sort_tile(7)
+        multiply_block(2, 0)
+        quantise_tile(6)
+        quantise_tile(7)
+        multiply_block(2, 1)
+        multiply_block(3, 0)
+        multiply_block(3, 1)

@@ -18,12 +18,14 @@ K = 2048
 N = 2048
 PASSES = K // K_PASS
 TOKEN_TILES = TOKENS // P
-PAIR = 2
-PAIRS = TOKEN_TILES // PAIR
 BANK = 512
+CHUNKS = N // BANK
 HALF = N // 2
 HALVES = N // HALF
-BANKS_PER_HALF = HALF // BANK
+HEAD_TURN_BANKS = [0, 1, 2, 3]
+TURN_BANKS = [0, 1]
+BIAS_BANKS = [4, 5]
+SUM_BANKS = [6, 7, 2, 3, 4, 5]
 
 FLOPS = 2 * TOKENS * K * N
 
@@ -35,9 +37,9 @@ def tile_tiledlinear_kernel(tc, x, weight_words, weight_scales, bias, out):
 
     with ExitStack() as ctx:
         keep = ctx.enter_context(tc.tile_pool(name="keep", bufs=1))
-        stage = ctx.enter_context(tc.tile_pool(name="stage", bufs=2))
-        results = ctx.enter_context(tc.tile_pool(name="results", bufs=TOKEN_TILES * (N // BANK)))
-        psum = ctx.enter_context(tc.psum_pool(name="psum", bufs=8))
+        stage = ctx.enter_context(tc.tile_pool(name="stage", bufs=3))
+        results = ctx.enter_context(tc.tile_pool(name="results", bufs=TOKEN_TILES * CHUNKS))
+        psum = ctx.enter_context(tc.psum_pool(name="psum", bufs=1))
         ctx.enter_context(tc.manual_schedule())
 
         x_raw = [keep.tile([P, K], BF16, name="x_raw%d" % m) for m in range(TOKEN_TILES)]
@@ -51,127 +53,215 @@ def tile_tiledlinear_kernel(tc, x, weight_words, weight_scales, bias, out):
             [keep.tile([P, HALF], U32, name="w_codes%d_%d" % (g, h), align_bytes=64) for h in range(HALVES)]
             for g in range(PASSES)
         ]
-        w_planes = keep.tile([P, N], U8, name="w_planes", align_bytes=64)
-        bias_rows = keep.tile([P, N], BF16, name="bias_rows")
-        bias_all = keep.tile([P, N], F32, name="bias_all")
-        ones = keep.tile([P, P], BF16, name="ones")
+        w_planes = [keep.tile([P, HALF], U8, name="w_planes%d" % h, align_bytes=64) for h in range(HALVES)]
+        bias_rows = keep.tile([P, BANK], BF16, name="bias_rows")
+        bias_all = keep.tile([P, N], BF16, name="bias_all")
         ident = keep.tile([P, P], F32, name="ident")
+        ident_bf = keep.tile([P, P], BF16, name="ident_bf")
+        dummy = keep.tile([P, 1], F32, name="dummy")
+        dummy_out = keep.tile([P, 1], F32, name="dummy_out")
 
-        nc.vector.memset(w_planes[:].bitcast(I32), 0)
-        nc.vector.memset(bias_rows[:], 0.0)
-        nc.vector.memset(ones[:], 1.0)
+        nc.vector.memset(dummy[:], 0.0)
+        nc.vector.memset(bias_rows[:].bitcast(I32), 0)
+        nc.vector.memset(w_planes[0][:].bitcast(I32), 0)
+        nc.vector.memset(w_planes[1][:].bitcast(I32), 0)
+        nc.scalar.dma_start(out=bias_rows[0:CHUNKS, :], in_=bias.rearrange("(r n) -> r n", r=CHUNKS))
+        nc.scalar.copy(out=dummy_out[:], in_=dummy[:])
         make_identity(nc, ident[:])
-        nc.scalar.dma_start(out=bias_rows[0:1, :], in_=bias.rearrange("(o n) -> o n", o=1))
+        nc.vector.tensor_copy(out=ident_bf[:], in_=ident[:])
 
         def load_x(m):
             nc.sync.dma_start(out=x_raw[m][:], in_=x_rows[m * P : (m + 1) * P, :])
 
-        def load_w_planes():
+        def load_w_planes(h):
             for quadrant in range(4):
                 nc.sync.dma_start(
-                    out=w_planes[32 * quadrant : 32 * quadrant + 16, :].bitcast(I32),
-                    in_=weight_scales[:, 4 * quadrant : 4 * quadrant + 4, :].bitcast(I32),
+                    out=w_planes[h][32 * quadrant : 32 * quadrant + 16, :].bitcast(I32),
+                    in_=weight_scales[:, 4 * quadrant : 4 * quadrant + 4, h * HALF : (h + 1) * HALF].bitcast(I32),
                 )
 
-        def load_w_half(h):
-            for g in range(PASSES):
-                w_bytes = weight_words[g].rearrange("p n t -> p (n t)")
-                nc.sync.dma_start(
-                    out=w_codes[g][h][:].bitcast(I32),
-                    in_=w_bytes[:, PACK * HALF * h : PACK * HALF * (h + 1)].bitcast(I32),
-                )
+        def load_w(g, first, last):
+            h = first // HALF
+            w_bytes = weight_words[g].rearrange("p n t -> p (n t)")
+            nc.sync.dma_start(
+                out=w_codes[g][h][:, first - h * HALF : last - h * HALF].bitcast(I32),
+                in_=w_bytes[:, PACK * first : PACK * last].bitcast(I32),
+            )
 
-        for m in range(2 * PAIR):
-            load_x(m)
-        load_w_planes()
-        load_w_half(0)
-        load_w_half(1)
-        for m in range(2 * PAIR, TOKEN_TILES):
+        load_x(0)
+        load_x(1)
+        load_w_planes(0)
+        load_w(0, 0, BANK)
+        load_w(0, BANK, HALF)
+        load_x(2)
+        for g in range(1, PASSES):
+            load_w(g, 0, HALF)
+        load_x(3)
+        load_w_planes(1)
+        for g in range(PASSES):
+            load_w(g, HALF, N)
+        for m in range(4, TOKEN_TILES):
             load_x(m)
 
         x_sorted = {}
+        turned = {}
+        grouped = {}
 
-        def sort_tile(m):
-            x_sorted[m] = stage.tile([P, PASSES, 2, P], F32, name="x_sorted")
+        def sort_words(m, s):
+            x_sorted[m, s] = stage.tile([P, 2, 2, P], F32, name="x_sorted%d" % s)
             nc.vector.tensor_copy(
-                out=x_sorted[m][:],
-                in_=x_raw[m][:].bitcast(F32).rearrange("t (g p u) -> t g u p", g=PASSES, u=2),
+                out=x_sorted[m, s][:],
+                in_=x_raw[m][:, s * 2 * K_PASS : (s + 1) * 2 * K_PASS]
+                .bitcast(F32)
+                .rearrange("t (g p u) -> t g u p", g=2, u=2),
             )
 
-        def quantise_tile(m):
-            grouped = stage.tile([P, PASSES, P, PACK], BF16, name="grouped", align_bytes=64)
-            for first_pass in range(0, PASSES, 2):
-                turned = psum.tile([P, 2, 2, P], F32, name="turned", tag="bank")
-                for j in range(2):
-                    g = first_pass + j
-                    for u in range(2):
-                        nc.tensor.transpose(turned[:, j, u, :], x_sorted[m][:, g, u, :], ident[:])
-                nc.scalar.copy(
-                    out=grouped[:, first_pass : first_pass + 2, :, :].bitcast(F32),
-                    in_=turned[:].rearrange("p j u t -> p j t u"),
-                )
+        def turn(m, s):
+            banks = HEAD_TURN_BANKS if m < 2 else TURN_BANKS
+            bank = banks[len(turned) % len(banks)]
+            turned[m, s] = psum.tile([P, 2, 2, P], F32, name="turned", tag="bank%d" % bank)
+            for j in range(2):
+                for u in range(2):
+                    nc.tensor.transpose(turned[m, s][:, j, u, :], x_sorted[m, s][:, j, u, :], ident[:])
+
+        def lay(m, s, copy):
+            grouped[m, s] = stage.tile([P, 2, P, PACK], BF16, name="grouped%d" % s, align_bytes=64)
+            copy(
+                out=grouped[m, s][:].bitcast(F32),
+                in_=turned[m, s][:].rearrange("p j u t -> p j t u"),
+            )
+
+        def quantise(m, s):
+            cols = slice(s * 2 * P, (s + 1) * 2 * P)
             nc.vector.quantize_mx(
-                out=x_codes[m][:].bitcast(FP8X4),
-                scales=x_planes[m][:],
-                in_=grouped[:].rearrange("p g t j -> p (g t j)"),
+                out=x_codes[m][:, cols].bitcast(FP8X4),
+                scales=x_planes[m][:, cols],
+                in_=grouped[m, s][:].rearrange("p g t j -> p (g t j)"),
             )
 
-        def spread_bias():
-            for c in range(N // BANK):
-                cols = slice(c * BANK, (c + 1) * BANK)
-                spread = psum.tile([P, BANK], F32, name="spread", tag="bank")
-                nc.tensor.matmul(spread[:], lhsT=ones[:], rhs=bias_rows[:, cols], start=True, stop=True)
-                nc.scalar.copy(out=bias_all[:, cols], in_=spread[:])
+        bias_psum = {}
 
-        def multiply_block(q, h):
-            groups = [(i, c) for i in range(PAIR) for c in range(BANKS_PER_HALF)]
-            if q == 0:
-                order = [(g, i, c) for g in range(PASSES) for (i, c) in groups]
-            else:
-                order = [(g, i, c) for (i, c) in groups for g in range(PASSES)]
-            acc = {}
-            for i, c in groups:
-                acc[i, c] = psum.tile([P, BANK], F32, name="acc%d%d" % (i, c), tag="bank")
-            for g, i, c in order:
-                m = PAIR * q + i
+        def spread_bias(b):
+            bias_psum[b] = psum.tile([P, 2 * BANK], BF16, name="bias_psum", tag="bank%d" % BIAS_BANKS[b])
+            for j in range(2):
+                r = 2 * b + j
+                nc.tensor.matmul(
+                    bias_psum[b][:, j * BANK : (j + 1) * BANK],
+                    lhsT=ident_bf[:, r : r + 1].to_broadcast([P, P]),
+                    rhs=bias_rows[:],
+                    start=True,
+                    stop=True,
+                )
+
+        def keep_bias(b):
+            nc.scalar.copy(out=bias_all[:, b * 2 * BANK : (b + 1) * 2 * BANK], in_=bias_psum[b][:])
+
+        sums = {}
+
+        def multiply(m, c, passes):
+            h, col = divmod(c * BANK, HALF)
+            if passes[0] == 0:
+                bank = SUM_BANKS[len(sums) % len(SUM_BANKS)]
+                sums[m, c] = psum.tile([P, BANK], F32, name="sums", tag="bank%d" % bank)
+            for g in passes:
                 nc.tensor.matmul_mx(
-                    out=acc[i, c][:],
+                    out=sums[m, c][:],
                     lhsT=x_codes[m][:, g * P : (g + 1) * P].bitcast(FP8X4),
                     lhsT_scale=x_planes[m][:, g * P : (g + 1) * P],
-                    rhs=w_codes[g][h][:, c * BANK : (c + 1) * BANK].bitcast(FP8X4),
-                    rhs_scale=w_planes[4 * g : P, h * HALF + c * BANK : h * HALF + (c + 1) * BANK],
+                    rhs=w_codes[g][h][:, col : col + BANK].bitcast(FP8X4),
+                    rhs_scale=w_planes[h][4 * g : P, col : col + BANK],
                     start=(g == 0),
                     stop=(g == PASSES - 1),
                 )
-            for i, c in groups:
-                m = PAIR * q + i
-                n_cols = slice(h * HALF + c * BANK, h * HALF + (c + 1) * BANK)
-                result = results.tile([P, BANK], F32, name="result")
-                nc.vector.tensor_tensor(out=result[:], in0=acc[i, c][:], in1=bias_all[:, n_cols], op=mybir.AluOpType.add)
-                nc.sync.dma_start(out=out_rows[m * P : (m + 1) * P, n_cols], in_=result[:])
 
-        sort_tile(0)
-        sort_tile(1)
-        quantise_tile(0)
-        sort_tile(2)
-        quantise_tile(1)
-        spread_bias()
-        sort_tile(3)
-        quantise_tile(2)
-        quantise_tile(3)
-        multiply_block(0, 0)
-        multiply_block(1, 0)
-        sort_tile(4)
-        sort_tile(5)
-        multiply_block(0, 1)
-        quantise_tile(4)
-        quantise_tile(5)
-        multiply_block(1, 1)
-        sort_tile(6)
-        sort_tile(7)
-        multiply_block(2, 0)
-        quantise_tile(6)
-        quantise_tile(7)
-        multiply_block(2, 1)
-        multiply_block(3, 0)
-        multiply_block(3, 1)
+        def finish(m, c):
+            n_cols = slice(c * BANK, (c + 1) * BANK)
+            result = results.tile([P, BANK], F32, name="result")
+            nc.vector.tensor_tensor(out=result[:], in0=sums[m, c][:], in1=bias_all[:, n_cols], op=mybir.AluOpType.add)
+            nc.sync.dma_start(out=out_rows[m * P : (m + 1) * P, n_cols], in_=result[:])
+
+        on_scalar = nc.scalar.copy
+        every_pass = list(range(PASSES))
+
+        on_vector = nc.vector.tensor_copy
+        for b in range(2):
+            spread_bias(b)
+            keep_bias(b)
+        for s in range(2):
+            sort_words(0, s)
+        for s in range(2):
+            turn(0, s)
+        lay(0, 0, on_scalar)
+        for s in range(2):
+            sort_words(1, s)
+        lay(0, 1, on_vector)
+        for s in range(2):
+            turn(1, s)
+        for s in range(2):
+            lay(1, s, on_scalar)
+        for s in range(2):
+            quantise(0, s)
+        for s in range(2):
+            quantise(1, s)
+        for c in range(2):
+            for m in range(2):
+                multiply(m, c, [0])
+        for s in range(2):
+            sort_words(2, s)
+        for s in range(2):
+            turn(2, s)
+            lay(2, s, on_scalar)
+        for s in range(2):
+            quantise(2, s)
+        for m in range(2):
+            for c in range(2):
+                multiply(m, c, [1])
+        for c in range(2):
+            multiply(2, c, [0, 1])
+        sort_words(3, 0)
+        sort_words(3, 1)
+        for m in range(2):
+            for c in range(2):
+                multiply(m, c, [2])
+        for s in range(2):
+            turn(3, s)
+            lay(3, s, on_scalar)
+        for c in range(2):
+            multiply(2, c, [2])
+        for s in range(2):
+            quantise(3, s)
+        for m in range(3):
+            for c in range(2):
+                multiply(m, c, [3])
+                finish(m, c)
+
+        def run(m, c):
+            multiply(m, c, every_pass)
+            finish(m, c)
+
+        run(3, 0)
+        run(3, 1)
+        for m in range(2):
+            run(m, 2)
+            run(m, 3)
+        for s in range(2):
+            sort_words(4, s)
+        run(2, 2)
+        run(2, 3)
+        for m in range(3, TOKEN_TILES):
+            chunks = [2, 3] if m == 3 else [0, 1, 2, 3]
+            last = m == TOKEN_TILES - 1
+            if m + 2 < TOKEN_TILES:
+                for s in range(2):
+                    sort_words(m + 2, s)
+            if not last:
+                for s in range(2):
+                    turn(m + 1, s)
+                    lay(m + 1, s, on_scalar)
+            run(m, chunks[0])
+            if not last:
+                for s in range(2):
+                    quantise(m + 1, s)
+            run(m, chunks[1])
+            for c in chunks[2:]:
+                run(m, c)

@@ -53,7 +53,7 @@ def tile_tiledlinear_kernel(tc, x, weight_words, weight_scales, bias, out):
             [keep.tile([P, HALF], U32, name="w_codes%d_%d" % (g, h), align_bytes=64) for h in range(HALVES)]
             for g in range(PASSES)
         ]
-        w_planes = [keep.tile([P, HALF], U8, name="w_planes%d" % h, align_bytes=64) for h in range(HALVES)]
+        w_planes = keep.tile([P, N], U8, name="w_planes", align_bytes=64)
         bias_rows = keep.tile([P, BANK], BF16, name="bias_rows")
         bias_all = keep.tile([P, N], BF16, name="bias_all")
         ident = keep.tile([P, P], F32, name="ident")
@@ -61,10 +61,9 @@ def tile_tiledlinear_kernel(tc, x, weight_words, weight_scales, bias, out):
         dummy = keep.tile([P, 1], F32, name="dummy")
         dummy_out = keep.tile([P, 1], F32, name="dummy_out")
 
+        nc.vector.memset(w_planes[:].bitcast(I32), 0)
         nc.vector.memset(dummy[:], 0.0)
         nc.vector.memset(bias_rows[:].bitcast(I32), 0)
-        nc.vector.memset(w_planes[0][:].bitcast(I32), 0)
-        nc.vector.memset(w_planes[1][:].bitcast(I32), 0)
         nc.scalar.dma_start(out=bias_rows[0:CHUNKS, :], in_=bias.rearrange("(r n) -> r n", r=CHUNKS))
         nc.scalar.copy(out=dummy_out[:], in_=dummy[:])
         make_identity(nc, ident[:])
@@ -73,11 +72,11 @@ def tile_tiledlinear_kernel(tc, x, weight_words, weight_scales, bias, out):
         def load_x(m):
             nc.sync.dma_start(out=x_raw[m][:], in_=x_rows[m * P : (m + 1) * P, :])
 
-        def load_w_planes(h):
+        def load_w_planes():
             for quadrant in range(4):
                 nc.sync.dma_start(
-                    out=w_planes[h][32 * quadrant : 32 * quadrant + 16, :].bitcast(I32),
-                    in_=weight_scales[:, 4 * quadrant : 4 * quadrant + 4, h * HALF : (h + 1) * HALF].bitcast(I32),
+                    out=w_planes[32 * quadrant : 32 * quadrant + 16, :].bitcast(I32),
+                    in_=weight_scales[:, 4 * quadrant : 4 * quadrant + 4, :].bitcast(I32),
                 )
 
         def load_w(g, first, last):
@@ -90,14 +89,13 @@ def tile_tiledlinear_kernel(tc, x, weight_words, weight_scales, bias, out):
 
         load_x(0)
         load_x(1)
-        load_w_planes(0)
+        load_w_planes()
         load_w(0, 0, BANK)
         load_w(0, BANK, HALF)
         load_x(2)
         for g in range(1, PASSES):
             load_w(g, 0, HALF)
         load_x(3)
-        load_w_planes(1)
         for g in range(PASSES):
             load_w(g, HALF, N)
         for m in range(4, TOKEN_TILES):
@@ -169,7 +167,7 @@ def tile_tiledlinear_kernel(tc, x, weight_words, weight_scales, bias, out):
                     lhsT=x_codes[m][:, g * P : (g + 1) * P].bitcast(FP8X4),
                     lhsT_scale=x_planes[m][:, g * P : (g + 1) * P],
                     rhs=w_codes[g][h][:, col : col + BANK].bitcast(FP8X4),
-                    rhs_scale=w_planes[h][4 * g : P, col : col + BANK],
+                    rhs_scale=w_planes[4 * g : P, c * BANK : (c + 1) * BANK],
                     start=(g == 0),
                     stop=(g == PASSES - 1),
                 )

@@ -22,6 +22,12 @@ BANK = 512
 CHUNKS = N // BANK
 HALF = N // 2
 HALVES = N // HALF
+WARM_MATMULS = 5
+
+SQUARE = 32
+QUADRANTS = P // SQUARE
+SQUARE_TILES = [5, 6, 7]
+
 HEAD_TURN_BANKS = [0, 1, 2, 3]
 TURN_BANKS = [0, 1]
 BIAS_BANKS = [4, 5]
@@ -42,7 +48,9 @@ def tile_tiledlinear_kernel(tc, x, weight_words, weight_scales, bias, out):
         psum = ctx.enter_context(tc.psum_pool(name="psum", bufs=1))
         ctx.enter_context(tc.manual_schedule())
 
-        x_raw = [keep.tile([P, K], BF16, name="x_raw%d" % m) for m in range(TOKEN_TILES)]
+        x_raw = [keep.tile([P, K], BF16, name="x_raw%d" % m) for m in range(SQUARE_TILES[0])]
+        runs = len(SQUARE_TILES) * QUADRANTS
+        square_raw = keep.tile([P, runs, PASSES, P], BF16, name="square_raw")
         x_codes = [
             keep.tile([P, PASSES * P], U32, name="x_codes%d" % m, align_bytes=64) for m in range(TOKEN_TILES)
         ]
@@ -58,12 +66,14 @@ def tile_tiledlinear_kernel(tc, x, weight_words, weight_scales, bias, out):
         bias_all = keep.tile([P, N], BF16, name="bias_all")
         ident = keep.tile([P, P], F32, name="ident")
         ident_bf = keep.tile([P, P], BF16, name="ident_bf")
+        warm = keep.tile([P, BANK], BF16, name="warm")
         dummy = keep.tile([P, 1], F32, name="dummy")
         dummy_out = keep.tile([P, 1], F32, name="dummy_out")
 
-        nc.vector.memset(w_planes[:].bitcast(I32), 0)
-        nc.vector.memset(dummy[:], 0.0)
         nc.vector.memset(bias_rows[:].bitcast(I32), 0)
+        nc.vector.memset(dummy[:], 0.0)
+        nc.vector.memset(warm[:].bitcast(I32), 0)
+        nc.vector.memset(w_planes[:].bitcast(I32), 0)
         nc.scalar.dma_start(out=bias_rows[0:CHUNKS, :], in_=bias.rearrange("(r n) -> r n", r=CHUNKS))
         nc.scalar.copy(out=dummy_out[:], in_=dummy[:])
         make_identity(nc, ident[:])
@@ -98,8 +108,15 @@ def tile_tiledlinear_kernel(tc, x, weight_words, weight_scales, bias, out):
         load_x(3)
         for g in range(PASSES):
             load_w(g, HALF, N)
-        for m in range(4, TOKEN_TILES):
-            load_x(m)
+        load_x(4)
+        square_rows = x_rows[SQUARE_TILES[0] * P : TOKENS, :]
+        for g in range(PASSES):
+            for q in (0, 2, 1, 3):
+                first = g * K_PASS + q * P
+                nc.sync.dma_start(
+                    out=square_raw[SQUARE * q : SQUARE * (q + 1), :, g, :],
+                    in_=square_rows[:, first : first + P].rearrange("(r j) c -> j r c", j=SQUARE),
+                )
 
         x_sorted = {}
         turned = {}
@@ -135,6 +152,46 @@ def tile_tiledlinear_kernel(tc, x, weight_words, weight_scales, bias, out):
                 out=x_codes[m][:, cols].bitcast(FP8X4),
                 scales=x_planes[m][:, cols],
                 in_=grouped[m, s][:].rearrange("p g t j -> p (g t j)"),
+            )
+
+        square_sorted = {}
+        square_turned = {}
+        square_grouped = {}
+
+        def sort_squares(m, s):
+            first = (m - SQUARE_TILES[0]) * QUADRANTS + 2 * s
+            if s == 0:
+                square_sorted[m] = stage.tile([P, 2, K_PASS], F32, name="square_sorted", align_bytes=64)
+            nc.scalar.copy(
+                out=square_sorted[m][:, s, :].rearrange("p (b u i) -> p b u i", u=2, i=SQUARE),
+                in_=square_raw[:, first : first + 2, :, :]
+                .rearrange("p r g c -> p (r g c)")
+                .bitcast(F32)
+                .rearrange("p (b i u) -> p b u i", u=2, i=SQUARE),
+            )
+
+        def turn_squares(m, s):
+            if s == 0:
+                square_turned[m] = stage.tile([P, 2, K_PASS], F32, name="square_turned", align_bytes=64)
+            nc.vector.transpose(out=square_turned[m][:, s, :], in_=square_sorted[m][:, s, :])
+
+        def lay_squares(m, s):
+            if s == 0:
+                square_grouped[m] = stage.tile([P, PASSES, P, PACK], BF16, name="square_grouped", align_bytes=64)
+            words = square_turned[m][:].rearrange("p s (r g u j) -> p (s r) g u j", r=2, g=PASSES, u=2)
+            grouped_words = square_grouped[m][:].rearrange("p g t j -> p g (t j)").bitcast(F32)
+            for g in range(2 * s, 2 * s + 2):
+                nc.scalar.copy(
+                    out=grouped_words[:, g, :].rearrange("p (r j u) -> p r j u", r=QUADRANTS, u=2),
+                    in_=words[:, :, g, :, :].rearrange("p r u j -> p r j u"),
+                )
+
+        def quantise_squares(m, s):
+            cols = slice(s * 2 * P, (s + 1) * 2 * P)
+            nc.vector.quantize_mx(
+                out=x_codes[m][:, cols].bitcast(FP8X4),
+                scales=x_planes[m][:, cols],
+                in_=square_grouped[m][:, 2 * s : 2 * s + 2, :, :].rearrange("p g t j -> p (g t j)"),
             )
 
         bias_psum = {}
@@ -182,19 +239,21 @@ def tile_tiledlinear_kernel(tc, x, weight_words, weight_scales, bias, out):
         every_pass = list(range(PASSES))
 
         on_vector = nc.vector.tensor_copy
-        for b in range(2):
-            spread_bias(b)
-            keep_bias(b)
+        warm_psum = psum.tile([P, BANK], F32, name="warm_psum", tag="bank%d" % SUM_BANKS[0])
+        for i in range(WARM_MATMULS):
+            nc.tensor.matmul(warm_psum[:], lhsT=warm[:, 0:P], rhs=warm[:], start=True, stop=True)
         for s in range(2):
             sort_words(0, s)
         for s in range(2):
             turn(0, s)
         lay(0, 0, on_scalar)
+        spread_bias(0)
         for s in range(2):
             sort_words(1, s)
         lay(0, 1, on_vector)
         for s in range(2):
             turn(1, s)
+        spread_bias(1)
         for s in range(2):
             lay(1, s, on_scalar)
         for s in range(2):
@@ -206,6 +265,8 @@ def tile_tiledlinear_kernel(tc, x, weight_words, weight_scales, bias, out):
                 multiply(m, c, [0])
         for s in range(2):
             sort_words(2, s)
+        for b in range(2):
+            keep_bias(b)
         for s in range(2):
             turn(2, s)
             lay(2, s, on_scalar)
@@ -239,27 +300,36 @@ def tile_tiledlinear_kernel(tc, x, weight_words, weight_scales, bias, out):
 
         run(3, 0)
         run(3, 1)
-        for m in range(2):
-            run(m, 2)
-            run(m, 3)
+        run(0, 2)
+        run(0, 3)
+        run(1, 2)
         for s in range(2):
             sort_words(4, s)
+        run(1, 3)
         run(2, 2)
         run(2, 3)
-        for m in range(3, TOKEN_TILES):
-            chunks = [2, 3] if m == 3 else [0, 1, 2, 3]
-            last = m == TOKEN_TILES - 1
-            if m + 2 < TOKEN_TILES:
+        for s in range(2):
+            turn(4, s)
+            lay(4, s, on_scalar)
+        multiply(3, 2, every_pass)
+        for s in range(2):
+            quantise(4, s)
+        finish(3, 2)
+        run(3, 3)
+        for m in range(4, TOKEN_TILES):
+            ahead = m + 1
+            if ahead < TOKEN_TILES:
                 for s in range(2):
-                    sort_words(m + 2, s)
-            if not last:
+                    sort_squares(ahead, s)
+                    turn_squares(ahead, s)
+                run(m, 0)
                 for s in range(2):
-                    turn(m + 1, s)
-                    lay(m + 1, s, on_scalar)
-            run(m, chunks[0])
-            if not last:
+                    lay_squares(ahead, s)
+                run(m, 1)
                 for s in range(2):
-                    quantise(m + 1, s)
-            run(m, chunks[1])
-            for c in chunks[2:]:
-                run(m, c)
+                    quantise_squares(ahead, s)
+                run(m, 2)
+                run(m, 3)
+            else:
+                for c in range(CHUNKS):
+                    run(m, c)

@@ -23,15 +23,17 @@ CHUNKS = N // BANK
 HALF = N // 2
 HALVES = N // HALF
 WARM_MATMULS = 5
+UNSORTED_TILES = 3
 
 SQUARE = 32
 QUADRANTS = P // SQUARE
-SQUARE_TILES = [5, 6, 7]
+SQUARE_GROUPS = [[4, 5], [6, 7]]
+PLAIN_TILES = SQUARE_GROUPS[0][0]
 
 HEAD_TURN_BANKS = [0, 1, 2, 3]
 TURN_BANKS = [0, 1]
 BIAS_BANKS = [4, 5]
-SUM_BANKS = [6, 7, 2, 3, 4, 5]
+SUM_BANKS = [6, 7, 2, 3, 4, 5, 0, 1]
 
 FLOPS = 2 * TOKENS * K * N
 
@@ -48,9 +50,11 @@ def tile_tiledlinear_kernel(tc, x, weight_words, weight_scales, bias, out):
         psum = ctx.enter_context(tc.psum_pool(name="psum", bufs=1))
         ctx.enter_context(tc.manual_schedule())
 
-        x_raw = [keep.tile([P, K], BF16, name="x_raw%d" % m) for m in range(SQUARE_TILES[0])]
-        runs = len(SQUARE_TILES) * QUADRANTS
-        square_raw = keep.tile([P, runs, PASSES, P], BF16, name="square_raw")
+        x_raw = [keep.tile([P, K], BF16, name="x_raw%d" % m) for m in range(PLAIN_TILES)]
+        square_raw = []
+        for i, tiles in enumerate(SQUARE_GROUPS):
+            raw = keep.tile([P, len(tiles) * QUADRANTS, PASSES, P], BF16, name="square_raw%d" % i)
+            square_raw.append(raw)
         x_codes = [
             keep.tile([P, PASSES * P], U32, name="x_codes%d" % m, align_bytes=64) for m in range(TOKEN_TILES)
         ]
@@ -61,7 +65,7 @@ def tile_tiledlinear_kernel(tc, x, weight_words, weight_scales, bias, out):
             [keep.tile([P, HALF], U32, name="w_codes%d_%d" % (g, h), align_bytes=64) for h in range(HALVES)]
             for g in range(PASSES)
         ]
-        w_planes = keep.tile([P, N], U8, name="w_planes", align_bytes=64)
+        w_planes = [keep.tile([P, HALF], U8, name="w_planes%d" % h, align_bytes=64) for h in range(HALVES)]
         bias_rows = keep.tile([P, BANK], BF16, name="bias_rows")
         bias_all = keep.tile([P, N], BF16, name="bias_all")
         ident = keep.tile([P, P], F32, name="ident")
@@ -73,8 +77,8 @@ def tile_tiledlinear_kernel(tc, x, weight_words, weight_scales, bias, out):
         nc.vector.memset(bias_rows[:].bitcast(I32), 0)
         nc.vector.memset(dummy[:], 0.0)
         nc.vector.memset(warm[:].bitcast(I32), 0)
-        nc.vector.memset(w_planes[:].bitcast(I32), 0)
-        nc.scalar.dma_start(out=bias_rows[0:CHUNKS, :], in_=bias.rearrange("(r n) -> r n", r=CHUNKS))
+        for h in range(HALVES):
+            nc.vector.memset(w_planes[h][:].bitcast(I32), 0)
         nc.scalar.copy(out=dummy_out[:], in_=dummy[:])
         make_identity(nc, ident[:])
         nc.vector.tensor_copy(out=ident_bf[:], in_=ident[:])
@@ -82,11 +86,11 @@ def tile_tiledlinear_kernel(tc, x, weight_words, weight_scales, bias, out):
         def load_x(m):
             nc.sync.dma_start(out=x_raw[m][:], in_=x_rows[m * P : (m + 1) * P, :])
 
-        def load_w_planes():
+        def load_w_planes(h):
             for quadrant in range(4):
                 nc.sync.dma_start(
-                    out=w_planes[32 * quadrant : 32 * quadrant + 16, :].bitcast(I32),
-                    in_=weight_scales[:, 4 * quadrant : 4 * quadrant + 4, :].bitcast(I32),
+                    out=w_planes[h][32 * quadrant : 32 * quadrant + 16, :].bitcast(I32),
+                    in_=weight_scales[:, 4 * quadrant : 4 * quadrant + 4, h * HALF : (h + 1) * HALF].bitcast(I32),
                 )
 
         def load_w(g, first, last):
@@ -97,26 +101,32 @@ def tile_tiledlinear_kernel(tc, x, weight_words, weight_scales, bias, out):
                 in_=w_bytes[:, PACK * first : PACK * last].bitcast(I32),
             )
 
-        load_x(0)
+        def load_squares(i, g, quadrants):
+            tiles = SQUARE_GROUPS[i]
+            rows = x_rows[tiles[0] * P : (tiles[-1] + 1) * P, :]
+            for q in quadrants:
+                first = g * K_PASS + q * P
+                nc.sync.dma_start(
+                    out=square_raw[i][SQUARE * q : SQUARE * (q + 1), :, g, :],
+                    in_=rows[:, first : first + P].rearrange("(r j) c -> j r c", j=SQUARE),
+                )
+
+        for s in range(2):
+            cols = slice(s * 2 * K_PASS, (s + 1) * 2 * K_PASS)
+            nc.sync.dma_start(out=x_raw[0][:, cols], in_=x_rows[0:P, cols])
         load_x(1)
-        load_w_planes()
+        nc.sync.dma_start(out=bias_rows[0:CHUNKS, :], in_=bias.rearrange("(r n) -> r n", r=CHUNKS))
+        load_w_planes(0)
         load_w(0, 0, BANK)
         load_w(0, BANK, HALF)
         load_x(2)
         for g in range(1, PASSES):
             load_w(g, 0, HALF)
         load_x(3)
+        load_w_planes(1)
         for g in range(PASSES):
             load_w(g, HALF, N)
-        load_x(4)
-        square_rows = x_rows[SQUARE_TILES[0] * P : TOKENS, :]
-        for g in range(PASSES):
-            for q in (0, 2, 1, 3):
-                first = g * K_PASS + q * P
-                nc.sync.dma_start(
-                    out=square_raw[SQUARE * q : SQUARE * (q + 1), :, g, :],
-                    in_=square_rows[:, first : first + P].rearrange("(r j) c -> j r c", j=SQUARE),
-                )
+            load_squares(0, g, [0, 2, 1, 3])
 
         x_sorted = {}
         turned = {}
@@ -137,7 +147,12 @@ def tile_tiledlinear_kernel(tc, x, weight_words, weight_scales, bias, out):
             turned[m, s] = psum.tile([P, 2, 2, P], F32, name="turned", tag="bank%d" % bank)
             for j in range(2):
                 for u in range(2):
-                    nc.tensor.transpose(turned[m, s][:, j, u, :], x_sorted[m, s][:, j, u, :], ident[:])
+                    if m < UNSORTED_TILES:
+                        first = (2 * s + j) * 2 * P + u
+                        words = x_raw[m][:].bitcast(F32)[:, first : first + 2 * P - u : 2]
+                    else:
+                        words = x_sorted[m, s][:, j, u, :]
+                    nc.tensor.transpose(turned[m, s][:, j, u, :], words, ident[:])
 
         def lay(m, s, copy):
             grouped[m, s] = stage.tile([P, 2, P, PACK], BF16, name="grouped%d" % s, align_bytes=64)
@@ -159,12 +174,13 @@ def tile_tiledlinear_kernel(tc, x, weight_words, weight_scales, bias, out):
         square_grouped = {}
 
         def sort_squares(m, s):
-            first = (m - SQUARE_TILES[0]) * QUADRANTS + 2 * s
+            i, offset = divmod(m - PLAIN_TILES, 2)
+            first = offset * QUADRANTS + 2 * s
             if s == 0:
                 square_sorted[m] = stage.tile([P, 2, K_PASS], F32, name="square_sorted", align_bytes=64)
             nc.scalar.copy(
                 out=square_sorted[m][:, s, :].rearrange("p (b u i) -> p b u i", u=2, i=SQUARE),
-                in_=square_raw[:, first : first + 2, :, :]
+                in_=square_raw[i][:, first : first + 2, :, :]
                 .rearrange("p r g c -> p (r g c)")
                 .bitcast(F32)
                 .rearrange("p (b i u) -> p b u i", u=2, i=SQUARE),
@@ -209,31 +225,41 @@ def tile_tiledlinear_kernel(tc, x, weight_words, weight_scales, bias, out):
                 )
 
         def keep_bias(b):
-            nc.scalar.copy(out=bias_all[:, b * 2 * BANK : (b + 1) * 2 * BANK], in_=bias_psum[b][:])
+            nc.vector.tensor_copy(out=bias_all[:, b * 2 * BANK : (b + 1) * 2 * BANK], in_=bias_psum[b][:])
 
         sums = {}
 
-        def multiply(m, c, passes):
+        def multiply(m, c, passes, parts=1):
             h, col = divmod(c * BANK, HALF)
             if passes[0] == 0:
                 bank = SUM_BANKS[len(sums) % len(SUM_BANKS)]
                 sums[m, c] = psum.tile([P, BANK], F32, name="sums", tag="bank%d" % bank)
-            for g in passes:
-                nc.tensor.matmul_mx(
-                    out=sums[m, c][:],
-                    lhsT=x_codes[m][:, g * P : (g + 1) * P].bitcast(FP8X4),
-                    lhsT_scale=x_planes[m][:, g * P : (g + 1) * P],
-                    rhs=w_codes[g][h][:, col : col + BANK].bitcast(FP8X4),
-                    rhs_scale=w_planes[4 * g : P, c * BANK : (c + 1) * BANK],
-                    start=(g == 0),
-                    stop=(g == PASSES - 1),
-                )
+            for part in range(parts):
+                first, last = part * BANK // parts, (part + 1) * BANK // parts
+                for g in passes:
+                    x_cols = slice(g * P, g * P + P)
+                    nc.tensor.matmul_mx(
+                        out=sums[m, c][:, first:last],
+                        lhsT=x_codes[m][:, x_cols].bitcast(FP8X4),
+                        lhsT_scale=x_planes[m][:, x_cols],
+                        rhs=w_codes[g][h][:, col + first : col + last].bitcast(FP8X4),
+                        rhs_scale=w_planes[h][4 * g : P, col + first : col + last],
+                        start=(g == 0),
+                        stop=(g == PASSES - 1),
+                    )
 
-        def finish(m, c):
-            n_cols = slice(c * BANK, (c + 1) * BANK)
+        def finish(m, c, parts=1):
             result = results.tile([P, BANK], F32, name="result")
-            nc.vector.tensor_tensor(out=result[:], in0=sums[m, c][:], in1=bias_all[:, n_cols], op=mybir.AluOpType.add)
-            nc.sync.dma_start(out=out_rows[m * P : (m + 1) * P, n_cols], in_=result[:])
+            for part in range(parts):
+                first, last = part * BANK // parts, (part + 1) * BANK // parts
+                n_cols = slice(c * BANK + first, c * BANK + last)
+                nc.vector.tensor_tensor(
+                    out=result[:, first:last],
+                    in0=sums[m, c][:, first:last],
+                    in1=bias_all[:, n_cols],
+                    op=mybir.AluOpType.add,
+                )
+                nc.sync.dma_start(out=out_rows[m * P : (m + 1) * P, n_cols], in_=result[:, first:last])
 
         on_scalar = nc.scalar.copy
         every_pass = list(range(PASSES))
@@ -242,94 +268,95 @@ def tile_tiledlinear_kernel(tc, x, weight_words, weight_scales, bias, out):
         warm_psum = psum.tile([P, BANK], F32, name="warm_psum", tag="bank%d" % SUM_BANKS[0])
         for i in range(WARM_MATMULS):
             nc.tensor.matmul(warm_psum[:], lhsT=warm[:, 0:P], rhs=warm[:], start=True, stop=True)
-        for s in range(2):
-            sort_words(0, s)
-        for s in range(2):
-            turn(0, s)
+        def both(m, passes):
+            for c in range(2):
+                multiply(m, c, passes)
+
+        turn(0, 0)
         lay(0, 0, on_scalar)
-        spread_bias(0)
-        for s in range(2):
-            sort_words(1, s)
+        turn(0, 1)
+        quantise(0, 0)
         lay(0, 1, on_vector)
-        for s in range(2):
-            turn(1, s)
+        quantise(0, 1)
+        spread_bias(0)
+        turn(1, 0)
+        lay(1, 0, on_scalar)
+        turn(1, 1)
+        lay(1, 1, on_scalar)
         spread_bias(1)
-        for s in range(2):
-            lay(1, s, on_scalar)
-        for s in range(2):
-            quantise(0, s)
-        for s in range(2):
-            quantise(1, s)
-        for c in range(2):
-            for m in range(2):
-                multiply(m, c, [0])
-        for s in range(2):
-            sort_words(2, s)
+        both(0, [0])
+        quantise(1, 0)
+        both(1, [0])
+        quantise(1, 1)
         for b in range(2):
             keep_bias(b)
-        for s in range(2):
-            turn(2, s)
-            lay(2, s, on_scalar)
+        turn(2, 0)
+        lay(2, 0, on_scalar)
+        turn(2, 1)
+        lay(2, 1, on_scalar)
+        both(0, [1])
+        both(1, [1])
         for s in range(2):
             quantise(2, s)
-        for m in range(2):
-            for c in range(2):
-                multiply(m, c, [1])
-        for c in range(2):
-            multiply(2, c, [0, 1])
-        sort_words(3, 0)
-        sort_words(3, 1)
-        for m in range(2):
-            for c in range(2):
-                multiply(m, c, [2])
+        both(2, [0, 1])
+        for s in range(2):
+            sort_words(3, s)
+        for m in range(3):
+            both(m, [2])
         for s in range(2):
             turn(3, s)
             lay(3, s, on_scalar)
-        for c in range(2):
-            multiply(2, c, [2])
+        both(0, [3])
         for s in range(2):
             quantise(3, s)
+        both(1, [3])
+        both(2, [3])
         for m in range(3):
             for c in range(2):
-                multiply(m, c, [3])
                 finish(m, c)
 
         def run(m, c):
             multiply(m, c, every_pass)
             finish(m, c)
 
-        run(3, 0)
-        run(3, 1)
-        run(0, 2)
-        run(0, 3)
-        run(1, 2)
-        for s in range(2):
-            sort_words(4, s)
-        run(1, 3)
+        def square_step(step, m):
+            if PLAIN_TILES <= m < TOKEN_TILES:
+                for s in range(2):
+                    step(m, s)
+
+        for c in range(2):
+            load_squares(1, 2 * c, [0, 2, 1, 3])
+            load_squares(1, 2 * c + 1, [0, 2, 1, 3])
+            run(3, c)
+        square_step(sort_squares, 4)
+        for g in every_pass:
+            for m in range(2):
+                for c in (2, 3):
+                    multiply(m, c, [g])
+                    if g == PASSES - 1:
+                        finish(m, c)
+            if g == 1:
+                square_step(turn_squares, 4)
+                square_step(lay_squares, 4)
+                square_step(sort_squares, 5)
         run(2, 2)
+        square_step(quantise_squares, 4)
+        square_step(turn_squares, 5)
         run(2, 3)
-        for s in range(2):
-            turn(4, s)
-            lay(4, s, on_scalar)
-        multiply(3, 2, every_pass)
-        for s in range(2):
-            quantise(4, s)
-        finish(3, 2)
+        square_step(lay_squares, 5)
+        square_step(sort_squares, 6)
+        run(3, 2)
+        square_step(quantise_squares, 5)
         run(3, 3)
-        for m in range(4, TOKEN_TILES):
-            ahead = m + 1
-            if ahead < TOKEN_TILES:
-                for s in range(2):
-                    sort_squares(ahead, s)
-                    turn_squares(ahead, s)
-                run(m, 0)
-                for s in range(2):
-                    lay_squares(ahead, s)
-                run(m, 1)
-                for s in range(2):
-                    quantise_squares(ahead, s)
-                run(m, 2)
+        for m in range(PLAIN_TILES, TOKEN_TILES):
+            run(m, 0)
+            square_step(turn_squares, m + 2)
+            run(m, 1)
+            square_step(lay_squares, m + 2)
+            square_step(sort_squares, m + 3)
+            run(m, 2)
+            square_step(quantise_squares, m + 2)
+            if m < TOKEN_TILES - 1:
                 run(m, 3)
-            else:
-                for c in range(CHUNKS):
-                    run(m, c)
+        multiply(TOKEN_TILES - 1, CHUNKS - 1, every_pass, 2)
+        finish(TOKEN_TILES - 1, CHUNKS - 1, 2)

@@ -25,15 +25,10 @@ HALVES = N // HALF
 WARM_MATMULS = 5
 UNSORTED_TILES = 3
 
-SQUARE = 32
-QUADRANTS = P // SQUARE
-SQUARE_GROUPS = [[4, 5], [6, 7]]
-PLAIN_TILES = SQUARE_GROUPS[0][0]
-
 HEAD_TURN_BANKS = [0, 1, 2, 3]
-TURN_BANKS = [0, 1]
 BIAS_BANKS = [4, 5]
-SUM_BANKS = [6, 7, 2, 3, 4, 5, 0, 1]
+BANKS = [6, 7, 2, 3, 4, 5, 0, 1]
+HEAD_TILES = 4
 
 FLOPS = 2 * TOKENS * K * N
 
@@ -45,16 +40,12 @@ def tile_tiledlinear_kernel(tc, x, weight_words, weight_scales, bias, out):
 
     with ExitStack() as ctx:
         keep = ctx.enter_context(tc.tile_pool(name="keep", bufs=1))
-        stage = ctx.enter_context(tc.tile_pool(name="stage", bufs=3))
+        stage = ctx.enter_context(tc.tile_pool(name="stage", bufs=4))
         results = ctx.enter_context(tc.tile_pool(name="results", bufs=TOKEN_TILES * CHUNKS))
         psum = ctx.enter_context(tc.psum_pool(name="psum", bufs=1))
         ctx.enter_context(tc.manual_schedule())
 
-        x_raw = [keep.tile([P, K], BF16, name="x_raw%d" % m) for m in range(PLAIN_TILES)]
-        square_raw = []
-        for i, tiles in enumerate(SQUARE_GROUPS):
-            raw = keep.tile([P, len(tiles) * QUADRANTS, PASSES, P], BF16, name="square_raw%d" % i)
-            square_raw.append(raw)
+        x_raw = [keep.tile([P, K], BF16, name="x_raw%d" % m) for m in range(TOKEN_TILES)]
         x_codes = [
             keep.tile([P, PASSES * P], U32, name="x_codes%d" % m, align_bytes=64) for m in range(TOKEN_TILES)
         ]
@@ -101,24 +92,13 @@ def tile_tiledlinear_kernel(tc, x, weight_words, weight_scales, bias, out):
                 in_=w_bytes[:, PACK * first : PACK * last].bitcast(I32),
             )
 
-        def load_squares(i, g, quadrants):
-            tiles = SQUARE_GROUPS[i]
-            rows = x_rows[tiles[0] * P : (tiles[-1] + 1) * P, :]
-            for q in quadrants:
-                first = g * K_PASS + q * P
-                nc.sync.dma_start(
-                    out=square_raw[i][SQUARE * q : SQUARE * (q + 1), :, g, :],
-                    in_=rows[:, first : first + P].rearrange("(r j) c -> j r c", j=SQUARE),
-                )
-
         for s in range(2):
             cols = slice(s * 2 * K_PASS, (s + 1) * 2 * K_PASS)
             nc.sync.dma_start(out=x_raw[0][:, cols], in_=x_rows[0:P, cols])
         load_x(1)
         nc.sync.dma_start(out=bias_rows[0:CHUNKS, :], in_=bias.rearrange("(r n) -> r n", r=CHUNKS))
         load_w_planes(0)
-        load_w(0, 0, BANK)
-        load_w(0, BANK, HALF)
+        load_w(0, 0, HALF)
         load_x(2)
         for g in range(1, PASSES):
             load_w(g, 0, HALF)
@@ -126,7 +106,14 @@ def tile_tiledlinear_kernel(tc, x, weight_words, weight_scales, bias, out):
         load_w_planes(1)
         for g in range(PASSES):
             load_w(g, HALF, N)
-            load_squares(0, g, [0, 2, 1, 3])
+        for m in range(4, TOKEN_TILES):
+            load_x(m)
+
+        taken = []
+
+        def next_bank():
+            taken.append(BANKS[len(taken) % len(BANKS)])
+            return taken[-1]
 
         x_sorted = {}
         turned = {}
@@ -142,8 +129,7 @@ def tile_tiledlinear_kernel(tc, x, weight_words, weight_scales, bias, out):
             )
 
         def turn(m, s):
-            banks = HEAD_TURN_BANKS if m < 2 else TURN_BANKS
-            bank = banks[len(turned) % len(banks)]
+            bank = HEAD_TURN_BANKS[(2 * m + s) % (4 if m < 2 else 2)] if m < HEAD_TILES else next_bank()
             turned[m, s] = psum.tile([P, 2, 2, P], F32, name="turned", tag="bank%d" % bank)
             for j in range(2):
                 for u in range(2):
@@ -169,47 +155,6 @@ def tile_tiledlinear_kernel(tc, x, weight_words, weight_scales, bias, out):
                 in_=grouped[m, s][:].rearrange("p g t j -> p (g t j)"),
             )
 
-        square_sorted = {}
-        square_turned = {}
-        square_grouped = {}
-
-        def sort_squares(m, s):
-            i, offset = divmod(m - PLAIN_TILES, 2)
-            first = offset * QUADRANTS + 2 * s
-            if s == 0:
-                square_sorted[m] = stage.tile([P, 2, K_PASS], F32, name="square_sorted", align_bytes=64)
-            nc.scalar.copy(
-                out=square_sorted[m][:, s, :].rearrange("p (b u i) -> p b u i", u=2, i=SQUARE),
-                in_=square_raw[i][:, first : first + 2, :, :]
-                .rearrange("p r g c -> p (r g c)")
-                .bitcast(F32)
-                .rearrange("p (b i u) -> p b u i", u=2, i=SQUARE),
-            )
-
-        def turn_squares(m, s):
-            if s == 0:
-                square_turned[m] = stage.tile([P, 2, K_PASS], F32, name="square_turned", align_bytes=64)
-            nc.vector.transpose(out=square_turned[m][:, s, :], in_=square_sorted[m][:, s, :])
-
-        def lay_squares(m, s):
-            if s == 0:
-                square_grouped[m] = stage.tile([P, PASSES, P, PACK], BF16, name="square_grouped", align_bytes=64)
-            words = square_turned[m][:].rearrange("p s (r g u j) -> p (s r) g u j", r=2, g=PASSES, u=2)
-            grouped_words = square_grouped[m][:].rearrange("p g t j -> p g (t j)").bitcast(F32)
-            for g in range(2 * s, 2 * s + 2):
-                nc.scalar.copy(
-                    out=grouped_words[:, g, :].rearrange("p (r j u) -> p r j u", r=QUADRANTS, u=2),
-                    in_=words[:, :, g, :, :].rearrange("p r u j -> p r j u"),
-                )
-
-        def quantise_squares(m, s):
-            cols = slice(s * 2 * P, (s + 1) * 2 * P)
-            nc.vector.quantize_mx(
-                out=x_codes[m][:, cols].bitcast(FP8X4),
-                scales=x_planes[m][:, cols],
-                in_=square_grouped[m][:, 2 * s : 2 * s + 2, :, :].rearrange("p g t j -> p (g t j)"),
-            )
-
         bias_psum = {}
 
         def spread_bias(b):
@@ -232,8 +177,7 @@ def tile_tiledlinear_kernel(tc, x, weight_words, weight_scales, bias, out):
         def multiply(m, c, passes, parts=1):
             h, col = divmod(c * BANK, HALF)
             if passes[0] == 0:
-                bank = SUM_BANKS[len(sums) % len(SUM_BANKS)]
-                sums[m, c] = psum.tile([P, BANK], F32, name="sums", tag="bank%d" % bank)
+                sums[m, c] = psum.tile([P, BANK], F32, name="sums", tag="bank%d" % next_bank())
             for part in range(parts):
                 first, last = part * BANK // parts, (part + 1) * BANK // parts
                 for g in passes:
@@ -263,9 +207,10 @@ def tile_tiledlinear_kernel(tc, x, weight_words, weight_scales, bias, out):
 
         on_scalar = nc.scalar.copy
         every_pass = list(range(PASSES))
+        every_chunk = list(range(CHUNKS))
 
         on_vector = nc.vector.tensor_copy
-        warm_psum = psum.tile([P, BANK], F32, name="warm_psum", tag="bank%d" % SUM_BANKS[0])
+        warm_psum = psum.tile([P, BANK], F32, name="warm_psum", tag="bank%d" % BANKS[0])
         for i in range(WARM_MATMULS):
             nc.tensor.matmul(warm_psum[:], lhsT=warm[:, 0:P], rhs=warm[:], start=True, stop=True)
         def both(m, passes):
@@ -319,44 +264,46 @@ def tile_tiledlinear_kernel(tc, x, weight_words, weight_scales, bias, out):
             multiply(m, c, every_pass)
             finish(m, c)
 
-        def square_step(step, m):
-            if PLAIN_TILES <= m < TOKEN_TILES:
+        def prepare(step, tiles):
+            for m in tiles:
                 for s in range(2):
                     step(m, s)
 
-        for c in range(2):
-            load_squares(1, 2 * c, [0, 2, 1, 3])
-            load_squares(1, 2 * c + 1, [0, 2, 1, 3])
-            run(3, c)
-        square_step(sort_squares, 4)
+        def raise_tiles(tiles):
+            for m in tiles:
+                for s in range(2):
+                    turn(m, s)
+                    lay(m, s, on_scalar)
+
+        run(3, 0)
+        run(3, 1)
+        prepare(sort_words, [4, 5])
         for g in every_pass:
             for m in range(2):
                 for c in (2, 3):
                     multiply(m, c, [g])
                     if g == PASSES - 1:
                         finish(m, c)
-            if g == 1:
-                square_step(turn_squares, 4)
-                square_step(lay_squares, 4)
-                square_step(sort_squares, 5)
+        raise_tiles([4, 5])
         run(2, 2)
-        square_step(quantise_squares, 4)
-        square_step(turn_squares, 5)
+        prepare(quantise, [4])
         run(2, 3)
-        square_step(lay_squares, 5)
-        square_step(sort_squares, 6)
         run(3, 2)
-        square_step(quantise_squares, 5)
+        prepare(quantise, [5])
         run(3, 3)
-        for m in range(PLAIN_TILES, TOKEN_TILES):
-            run(m, 0)
-            square_step(turn_squares, m + 2)
-            run(m, 1)
-            square_step(lay_squares, m + 2)
-            square_step(sort_squares, m + 3)
-            run(m, 2)
-            square_step(quantise_squares, m + 2)
-            if m < TOKEN_TILES - 1:
-                run(m, 3)
-        multiply(TOKEN_TILES - 1, CHUNKS - 1, every_pass, 2)
-        finish(TOKEN_TILES - 1, CHUNKS - 1, 2)
+        prepare(sort_words, [6, 7])
+        for c in every_chunk:
+            run(4, c)
+        raise_tiles([6, 7])
+        run(5, 0)
+        run(5, 1)
+        prepare(quantise, [6])
+        run(5, 2)
+        prepare(quantise, [7])
+        run(5, 3)
+        for c in every_chunk:
+            run(6, c)
+        for c in every_chunk[:-1]:
+            run(7, c)
+        multiply(7, CHUNKS - 1, every_pass, 2)
+        finish(7, CHUNKS - 1, 2)

@@ -25,6 +25,10 @@ HALVES = N // HALF
 WARM_MATMULS = 5
 UNSORTED_TILES = 3
 
+SQUARE = 32
+QUADRANTS = P // SQUARE
+PLAIN_TILES = 6
+
 HEAD_TURN_BANKS = [0, 1, 2, 3]
 BIAS_BANKS = [4, 5]
 BANKS = [6, 7, 2, 3, 4, 5, 0, 1]
@@ -45,7 +49,9 @@ def tile_tiledlinear_kernel(tc, x, weight_words, weight_scales, bias, out):
         psum = ctx.enter_context(tc.psum_pool(name="psum", bufs=1))
         ctx.enter_context(tc.manual_schedule())
 
-        x_raw = [keep.tile([P, K], BF16, name="x_raw%d" % m) for m in range(TOKEN_TILES)]
+        x_raw = [keep.tile([P, K], BF16, name="x_raw%d" % m) for m in range(PLAIN_TILES)]
+        runs = (TOKEN_TILES - PLAIN_TILES) * QUADRANTS
+        square_raw = keep.tile([P, runs, PASSES, P], BF16, name="square_raw")
         x_codes = [
             keep.tile([P, PASSES * P], U32, name="x_codes%d" % m, align_bytes=64) for m in range(TOKEN_TILES)
         ]
@@ -106,8 +112,16 @@ def tile_tiledlinear_kernel(tc, x, weight_words, weight_scales, bias, out):
         load_w_planes(1)
         for g in range(PASSES):
             load_w(g, HALF, N)
-        for m in range(4, TOKEN_TILES):
+        for m in range(4, PLAIN_TILES):
             load_x(m)
+        square_rows = x_rows[PLAIN_TILES * P : TOKENS, :]
+        for g in range(PASSES):
+            for q in (0, 2, 1, 3):
+                first = g * K_PASS + q * P
+                nc.sync.dma_start(
+                    out=square_raw[SQUARE * q : SQUARE * (q + 1), :, g, :],
+                    in_=square_rows[:, first : first + P].rearrange("(r j) c -> j r c", j=SQUARE),
+                )
 
         taken = []
 
@@ -153,6 +167,46 @@ def tile_tiledlinear_kernel(tc, x, weight_words, weight_scales, bias, out):
                 out=x_codes[m][:, cols].bitcast(FP8X4),
                 scales=x_planes[m][:, cols],
                 in_=grouped[m, s][:].rearrange("p g t j -> p (g t j)"),
+            )
+
+        square_sorted = {}
+        square_turned = {}
+        square_grouped = {}
+
+        def sort_squares(m, s):
+            first = (m - PLAIN_TILES) * QUADRANTS + 2 * s
+            if s == 0:
+                square_sorted[m] = stage.tile([P, 2, K_PASS], F32, name="square_sorted", align_bytes=64)
+            nc.scalar.copy(
+                out=square_sorted[m][:, s, :].rearrange("p (b u i) -> p b u i", u=2, i=SQUARE),
+                in_=square_raw[:, first : first + 2, :, :]
+                .rearrange("p r g c -> p (r g c)")
+                .bitcast(F32)
+                .rearrange("p (b i u) -> p b u i", u=2, i=SQUARE),
+            )
+
+        def turn_squares(m, s):
+            if s == 0:
+                square_turned[m] = stage.tile([P, 2, K_PASS], F32, name="square_turned", align_bytes=64)
+            nc.vector.transpose(out=square_turned[m][:, s, :], in_=square_sorted[m][:, s, :])
+
+        def lay_squares(m, s):
+            if s == 0:
+                square_grouped[m] = stage.tile([P, PASSES, P, PACK], BF16, name="square_grouped", align_bytes=64)
+            words = square_turned[m][:].rearrange("p s (r g u j) -> p (s r) g u j", r=2, g=PASSES, u=2)
+            grouped_words = square_grouped[m][:].rearrange("p g t j -> p g (t j)").bitcast(F32)
+            for g in range(2 * s, 2 * s + 2):
+                nc.scalar.copy(
+                    out=grouped_words[:, g, :].rearrange("p (r j u) -> p r j u", r=QUADRANTS, u=2),
+                    in_=words[:, :, g, :, :].rearrange("p r u j -> p r j u"),
+                )
+
+        def quantise_squares(m, s):
+            cols = slice(s * 2 * P, (s + 1) * 2 * P)
+            nc.vector.quantize_mx(
+                out=x_codes[m][:, cols].bitcast(FP8X4),
+                scales=x_planes[m][:, cols],
+                in_=square_grouped[m][:, 2 * s : 2 * s + 2, :, :].rearrange("p g t j -> p (g t j)"),
             )
 
         bias_psum = {}
@@ -207,7 +261,6 @@ def tile_tiledlinear_kernel(tc, x, weight_words, weight_scales, bias, out):
 
         on_scalar = nc.scalar.copy
         every_pass = list(range(PASSES))
-        every_chunk = list(range(CHUNKS))
 
         on_vector = nc.vector.tensor_copy
         warm_psum = psum.tile([P, BANK], F32, name="warm_psum", tag="bank%d" % BANKS[0])
@@ -291,19 +344,19 @@ def tile_tiledlinear_kernel(tc, x, weight_words, weight_scales, bias, out):
         run(3, 2)
         prepare(quantise, [5])
         run(3, 3)
-        prepare(sort_words, [6, 7])
-        for c in every_chunk:
-            run(4, c)
-        raise_tiles([6, 7])
-        run(5, 0)
-        run(5, 1)
-        prepare(quantise, [6])
-        run(5, 2)
-        prepare(quantise, [7])
-        run(5, 3)
-        for c in every_chunk:
-            run(6, c)
-        for c in every_chunk[:-1]:
-            run(7, c)
+        prepare(sort_squares, [6, 7])
+        for m in range(4, TOKEN_TILES):
+            ahead = m + 2 if m + 2 < TOKEN_TILES else None
+            run(m, 0)
+            if m + 1 in (6, 7):
+                prepare(quantise_squares, [m + 1])
+            run(m, 1)
+            if ahead:
+                prepare(turn_squares, [ahead])
+            run(m, 2)
+            if ahead:
+                prepare(lay_squares, [ahead])
+            if m < TOKEN_TILES - 1:
+                run(m, 3)
         multiply(7, CHUNKS - 1, every_pass, 2)
         finish(7, CHUNKS - 1, 2)

@@ -23,15 +23,13 @@ CHUNKS = N // BANK
 HALF = N // 2
 HALVES = N // HALF
 WARM_MATMULS = 5
-UNSORTED_TILES = 3
 
 SQUARE = 32
 QUADRANTS = P // SQUARE
 PLAIN_TILES = 6
 
-HEAD_TURN_BANKS = [0, 1, 2, 3]
-BIAS_BANKS = [4, 5]
-BANKS = [6, 7, 2, 3, 4, 5, 0, 1]
+HEAD_TURN_BANKS = {(0, 0): 0, (1, 0): 1, (2, 0): 2, (0, 1): 0, (1, 1): 1, (2, 1): 5, (3, 0): 1, (3, 1): 5}
+BANKS = [6, 7, 3, 4, 2, 0, 1, 5]
 HEAD_TILES = 4
 
 FLOPS = 2 * TOKENS * K * N
@@ -63,25 +61,24 @@ def tile_tiledlinear_kernel(tc, x, weight_words, weight_scales, bias, out):
             for g in range(PASSES)
         ]
         w_planes = [keep.tile([P, HALF], U8, name="w_planes%d" % h, align_bytes=64) for h in range(HALVES)]
-        bias_rows = keep.tile([P, BANK], BF16, name="bias_rows")
-        bias_all = keep.tile([P, N], BF16, name="bias_all")
+        bias_all = [keep.tile([P, HALF], BF16, name="bias_all%d" % h) for h in range(HALVES)]
         ident = keep.tile([P, P], F32, name="ident")
-        ident_bf = keep.tile([P, P], BF16, name="ident_bf")
         warm = keep.tile([P, BANK], BF16, name="warm")
         dummy = keep.tile([P, 1], F32, name="dummy")
         dummy_out = keep.tile([P, 1], F32, name="dummy_out")
 
-        nc.vector.memset(bias_rows[:].bitcast(I32), 0)
-        nc.vector.memset(dummy[:], 0.0)
         nc.vector.memset(warm[:].bitcast(I32), 0)
+        nc.vector.memset(dummy[:], 0.0)
         for h in range(HALVES):
             nc.vector.memset(w_planes[h][:].bitcast(I32), 0)
         nc.scalar.copy(out=dummy_out[:], in_=dummy[:])
         make_identity(nc, ident[:])
-        nc.vector.tensor_copy(out=ident_bf[:], in_=ident[:])
 
         def load_x(m):
             nc.sync.dma_start(out=x_raw[m][:], in_=x_rows[m * P : (m + 1) * P, :])
+
+        def load_bias(h):
+            nc.sync.dma_start(out=bias_all[h][:], in_=bias[h * HALF : (h + 1) * HALF].partition_broadcast(P))
 
         def load_w_planes(h):
             for quadrant in range(4):
@@ -98,20 +95,27 @@ def tile_tiledlinear_kernel(tc, x, weight_words, weight_scales, bias, out):
                 in_=w_bytes[:, PACK * first : PACK * last].bitcast(I32),
             )
 
-        for s in range(2):
+        def load_x_half(m, s):
             cols = slice(s * 2 * K_PASS, (s + 1) * 2 * K_PASS)
-            nc.sync.dma_start(out=x_raw[0][:, cols], in_=x_rows[0:P, cols])
-        load_x(1)
-        nc.sync.dma_start(out=bias_rows[0:CHUNKS, :], in_=bias.rearrange("(r n) -> r n", r=CHUNKS))
+            nc.sync.dma_start(out=x_raw[m][:, cols], in_=x_rows[m * P : (m + 1) * P, cols])
+
+        load_x_half(0, 0)
+        load_x_half(1, 0)
         load_w_planes(0)
-        load_w(0, 0, HALF)
-        load_x(2)
-        for g in range(1, PASSES):
-            load_w(g, 0, HALF)
+        load_x_half(2, 0)
+        load_w(0, 0, BANK)
+        load_w(0, BANK, HALF)
+        load_w(1, 0, HALF)
+        for m in range(3):
+            load_x_half(m, 1)
+        load_w(2, 0, HALF)
         load_x(3)
+        load_w(3, 0, HALF)
+        load_bias(0)
         load_w_planes(1)
         for g in range(PASSES):
             load_w(g, HALF, N)
+        load_bias(1)
         for m in range(4, PLAIN_TILES):
             load_x(m)
         square_rows = x_rows[PLAIN_TILES * P : TOKENS, :]
@@ -143,11 +147,11 @@ def tile_tiledlinear_kernel(tc, x, weight_words, weight_scales, bias, out):
             )
 
         def turn(m, s):
-            bank = HEAD_TURN_BANKS[(2 * m + s) % (4 if m < 2 else 2)] if m < HEAD_TILES else next_bank()
+            bank = HEAD_TURN_BANKS[m, s] if m < HEAD_TILES else next_bank()
             turned[m, s] = psum.tile([P, 2, 2, P], F32, name="turned", tag="bank%d" % bank)
             for j in range(2):
                 for u in range(2):
-                    if m < UNSORTED_TILES:
+                    if (m, s) not in x_sorted:
                         first = (2 * s + j) * 2 * P + u
                         words = x_raw[m][:].bitcast(F32)[:, first : first + 2 * P - u : 2]
                     else:
@@ -209,23 +213,6 @@ def tile_tiledlinear_kernel(tc, x, weight_words, weight_scales, bias, out):
                 in_=square_grouped[m][:, 2 * s : 2 * s + 2, :, :].rearrange("p g t j -> p (g t j)"),
             )
 
-        bias_psum = {}
-
-        def spread_bias(b):
-            bias_psum[b] = psum.tile([P, 2 * BANK], BF16, name="bias_psum", tag="bank%d" % BIAS_BANKS[b])
-            for j in range(2):
-                r = 2 * b + j
-                nc.tensor.matmul(
-                    bias_psum[b][:, j * BANK : (j + 1) * BANK],
-                    lhsT=ident_bf[:, r : r + 1].to_broadcast([P, P]),
-                    rhs=bias_rows[:],
-                    start=True,
-                    stop=True,
-                )
-
-        def keep_bias(b):
-            nc.vector.tensor_copy(out=bias_all[:, b * 2 * BANK : (b + 1) * 2 * BANK], in_=bias_psum[b][:])
-
         sums = {}
 
         def multiply(m, c, passes, parts=1):
@@ -247,6 +234,7 @@ def tile_tiledlinear_kernel(tc, x, weight_words, weight_scales, bias, out):
                     )
 
         def finish(m, c, parts=1):
+            h, col = divmod(c * BANK, HALF)
             result = results.tile([P, BANK], F32, name="result")
             for part in range(parts):
                 first, last = part * BANK // parts, (part + 1) * BANK // parts
@@ -254,15 +242,15 @@ def tile_tiledlinear_kernel(tc, x, weight_words, weight_scales, bias, out):
                 nc.vector.tensor_tensor(
                     out=result[:, first:last],
                     in0=sums[m, c][:, first:last],
-                    in1=bias_all[:, n_cols],
+                    in1=bias_all[h][:, col + first : col + last],
                     op=mybir.AluOpType.add,
                 )
                 nc.sync.dma_start(out=out_rows[m * P : (m + 1) * P, n_cols], in_=result[:, first:last])
 
         on_scalar = nc.scalar.copy
+        on_vector = nc.vector.tensor_copy
         every_pass = list(range(PASSES))
 
-        on_vector = nc.vector.tensor_copy
         warm_psum = psum.tile([P, BANK], F32, name="warm_psum", tag="bank%d" % BANKS[0])
         for i in range(WARM_MATMULS):
             nc.tensor.matmul(warm_psum[:], lhsT=warm[:, 0:P], rhs=warm[:], start=True, stop=True)
@@ -270,35 +258,30 @@ def tile_tiledlinear_kernel(tc, x, weight_words, weight_scales, bias, out):
             for c in range(2):
                 multiply(m, c, passes)
 
-        turn(0, 0)
-        lay(0, 0, on_scalar)
-        turn(0, 1)
-        quantise(0, 0)
-        lay(0, 1, on_vector)
-        quantise(0, 1)
-        spread_bias(0)
-        turn(1, 0)
-        lay(1, 0, on_scalar)
-        turn(1, 1)
-        lay(1, 1, on_scalar)
-        spread_bias(1)
-        both(0, [0])
-        quantise(1, 0)
-        both(1, [0])
-        quantise(1, 1)
-        for b in range(2):
-            keep_bias(b)
-        turn(2, 0)
-        lay(2, 0, on_scalar)
-        turn(2, 1)
-        lay(2, 1, on_scalar)
+        for m in range(3):
+            turn(m, 0)
+            lay(m, 0, on_scalar)
+            quantise(m, 0)
+        for c in range(2):
+            for m in range(2):
+                multiply(m, c, [0])
+        multiply(2, 0, [0])
+        for m in range(3):
+            sort_words(m, 1)
         both(0, [1])
         both(1, [1])
-        for s in range(2):
-            quantise(2, s)
-        both(2, [0, 1])
+        turn(0, 1)
+        lay(0, 1, on_scalar)
+        turn(1, 1)
+        lay(1, 1, on_vector)
+        turn(2, 1)
+        lay(2, 1, on_scalar)
+        for m in range(3):
+            quantise(m, 1)
         for s in range(2):
             sort_words(3, s)
+        multiply(2, 0, [1])
+        multiply(2, 1, [0, 1])
         for m in range(3):
             both(m, [2])
         for s in range(2):

@@ -22,14 +22,14 @@ BANK = 512
 CHUNKS = N // BANK
 HALF = N // 2
 HALVES = N // HALF
-WARM_MATMULS = 5
+WARM_MATMULS = 4
 
 SQUARE = 32
 QUADRANTS = P // SQUARE
 PLAIN_TILES = 6
 
 HEAD_TURN_BANKS = {(0, 0): 0, (1, 0): 1, (2, 0): 2, (0, 1): 0, (1, 1): 1, (2, 1): 5, (3, 0): 1, (3, 1): 5}
-BANKS = [6, 7, 3, 4, 2, 0, 1, 5]
+BANKS = [6, 7, 3, 2, 4, 0, 1, 5]
 HEAD_TILES = 4
 
 FLOPS = 2 * TOKENS * K * N
@@ -61,7 +61,10 @@ def tile_tiledlinear_kernel(tc, x, weight_words, weight_scales, bias, out):
             for g in range(PASSES)
         ]
         w_planes = [keep.tile([P, HALF], U8, name="w_planes%d" % h, align_bytes=64) for h in range(HALVES)]
-        bias_all = [keep.tile([P, HALF], BF16, name="bias_all%d" % h) for h in range(HALVES)]
+        bias_part = keep.tile([P, N // SQUARE], BF16, name="bias_part")
+        bias_repeated = stage.tile([P, N // 2], F32, name="bias_repeated", tag="square_sorted", align_bytes=64)
+        bias_turned = stage.tile([P, N // 2], F32, name="bias_turned", tag="square_turned", align_bytes=64)
+        bias_all = keep.tile([P, N], BF16, name="bias_all")
         ident = keep.tile([P, P], F32, name="ident")
         warm = keep.tile([P, BANK], BF16, name="warm")
         dummy = keep.tile([P, 1], F32, name="dummy")
@@ -76,9 +79,6 @@ def tile_tiledlinear_kernel(tc, x, weight_words, weight_scales, bias, out):
 
         def load_x(m):
             nc.sync.dma_start(out=x_raw[m][:], in_=x_rows[m * P : (m + 1) * P, :])
-
-        def load_bias(h):
-            nc.sync.dma_start(out=bias_all[h][:], in_=bias[h * HALF : (h + 1) * HALF].partition_broadcast(P))
 
         def load_w_planes(h):
             for quadrant in range(4):
@@ -99,23 +99,24 @@ def tile_tiledlinear_kernel(tc, x, weight_words, weight_scales, bias, out):
             cols = slice(s * 2 * K_PASS, (s + 1) * 2 * K_PASS)
             nc.sync.dma_start(out=x_raw[m][:, cols], in_=x_rows[m * P : (m + 1) * P, cols])
 
-        load_x_half(0, 0)
-        load_x_half(1, 0)
-        load_w_planes(0)
+        for m in range(2):
+            load_x_half(m, 0)
+        for q in range(QUADRANTS):
+            nc.sync.dma_start(
+                out=bias_part[SQUARE * q : SQUARE * (q + 1), :], in_=bias.rearrange("(j c) -> j c", j=SQUARE)
+            )
         load_x_half(2, 0)
-        load_w(0, 0, BANK)
-        load_w(0, BANK, HALF)
+        load_w(0, 0, HALF)
+        load_w_planes(0)
         load_w(1, 0, HALF)
         for m in range(3):
             load_x_half(m, 1)
         load_w(2, 0, HALF)
         load_x(3)
         load_w(3, 0, HALF)
-        load_bias(0)
         load_w_planes(1)
         for g in range(PASSES):
             load_w(g, HALF, N)
-        load_bias(1)
         for m in range(4, PLAIN_TILES):
             load_x(m)
         square_rows = x_rows[PLAIN_TILES * P : TOKENS, :]
@@ -213,6 +214,21 @@ def tile_tiledlinear_kernel(tc, x, weight_words, weight_scales, bias, out):
                 in_=square_grouped[m][:, 2 * s : 2 * s + 2, :, :].rearrange("p g t j -> p (g t j)"),
             )
 
+        def repeat_bias():
+            nc.vector.tensor_copy(
+                out=bias_repeated[:].rearrange("p (b i) -> p b i", i=SQUARE),
+                in_=bias_part[:].bitcast(F32).unsqueeze(2).to_broadcast([P, SQUARE, SQUARE]),
+            )
+
+        def turn_bias():
+            nc.vector.transpose(out=bias_turned[:], in_=bias_repeated[:])
+
+        def sort_bias():
+            nc.scalar.copy(
+                out=bias_all[:].bitcast(F32).rearrange("p (j b) -> p j b", j=SQUARE),
+                in_=bias_turned[:].rearrange("p (b j) -> p j b", j=SQUARE),
+            )
+
         sums = {}
 
         def multiply(m, c, passes, parts=1):
@@ -234,7 +250,6 @@ def tile_tiledlinear_kernel(tc, x, weight_words, weight_scales, bias, out):
                     )
 
         def finish(m, c, parts=1):
-            h, col = divmod(c * BANK, HALF)
             result = results.tile([P, BANK], F32, name="result")
             for part in range(parts):
                 first, last = part * BANK // parts, (part + 1) * BANK // parts
@@ -242,7 +257,7 @@ def tile_tiledlinear_kernel(tc, x, weight_words, weight_scales, bias, out):
                 nc.vector.tensor_tensor(
                     out=result[:, first:last],
                     in0=sums[m, c][:, first:last],
-                    in1=bias_all[h][:, col + first : col + last],
+                    in1=bias_all[:, n_cols],
                     op=mybir.AluOpType.add,
                 )
                 nc.sync.dma_start(out=out_rows[m * P : (m + 1) * P, n_cols], in_=result[:, first:last])
@@ -252,20 +267,27 @@ def tile_tiledlinear_kernel(tc, x, weight_words, weight_scales, bias, out):
         every_pass = list(range(PASSES))
 
         warm_psum = psum.tile([P, BANK], F32, name="warm_psum", tag="bank%d" % BANKS[0])
-        for i in range(WARM_MATMULS):
-            nc.tensor.matmul(warm_psum[:], lhsT=warm[:, 0:P], rhs=warm[:], start=True, stop=True)
+
+        def warm_up(matmuls):
+            for i in range(matmuls):
+                nc.tensor.matmul(warm_psum[:], lhsT=warm[:, 0:P], rhs=warm[:], start=True, stop=True)
+
+        warm_up(WARM_MATMULS)
         def both(m, passes):
             for c in range(2):
                 multiply(m, c, passes)
 
+        repeat_bias()
         for m in range(3):
             turn(m, 0)
             lay(m, 0, on_scalar)
             quantise(m, 0)
+        warm_up(2)
         for c in range(2):
             for m in range(2):
                 multiply(m, c, [0])
         multiply(2, 0, [0])
+        turn_bias()
         for m in range(3):
             sort_words(m, 1)
         both(0, [1])
@@ -276,6 +298,7 @@ def tile_tiledlinear_kernel(tc, x, weight_words, weight_scales, bias, out):
         lay(1, 1, on_vector)
         turn(2, 1)
         lay(2, 1, on_scalar)
+        sort_bias()
         for m in range(3):
             quantise(m, 1)
         for s in range(2):

@@ -72,8 +72,8 @@ def tile_tiledlinear_kernel(tc, x, weight_words, weight_scales, bias, out):
 
         nc.vector.memset(warm[:].bitcast(I32), 0)
         nc.vector.memset(dummy[:], 0.0)
-        for h in range(HALVES):
-            nc.vector.memset(w_planes[h][:].bitcast(I32), 0)
+        nc.gpsimd.memset(w_planes[0][:].bitcast(I32), 0)
+        nc.vector.memset(w_planes[1][:].bitcast(I32), 0)
         nc.scalar.copy(out=dummy_out[:], in_=dummy[:])
         make_identity(nc, ident[:])
 
@@ -99,18 +99,18 @@ def tile_tiledlinear_kernel(tc, x, weight_words, weight_scales, bias, out):
             cols = slice(s * 2 * K_PASS, (s + 1) * 2 * K_PASS)
             nc.sync.dma_start(out=x_raw[m][:, cols], in_=x_rows[m * P : (m + 1) * P, cols])
 
-        for m in range(2):
-            load_x_half(m, 0)
-        for q in range(QUADRANTS):
-            nc.sync.dma_start(
-                out=bias_part[SQUARE * q : SQUARE * (q + 1), :], in_=bias.rearrange("(j c) -> j c", j=SQUARE)
-            )
-        load_x_half(2, 0)
-        load_w(0, 0, HALF)
+        load_x_half(0, 0)
         load_w_planes(0)
+        for m in (1, 2):
+            load_x_half(m, 0)
+        load_w(0, 0, HALF)
         load_w(1, 0, HALF)
         for m in range(3):
             load_x_half(m, 1)
+        nc.sync.dma_start(
+            out=bias_part[:],
+            in_=bias.rearrange("(j c) -> j c", j=SQUARE).unsqueeze(0).to_broadcast([QUADRANTS, SQUARE, N // SQUARE]),
+        )
         load_w(2, 0, HALF)
         load_x(3)
         load_w(3, 0, HALF)
@@ -224,7 +224,7 @@ def tile_tiledlinear_kernel(tc, x, weight_words, weight_scales, bias, out):
             nc.vector.transpose(out=bias_turned[:], in_=bias_repeated[:])
 
         def sort_bias():
-            nc.scalar.copy(
+            nc.vector.tensor_copy(
                 out=bias_all[:].bitcast(F32).rearrange("p (j b) -> p j b", j=SQUARE),
                 in_=bias_turned[:].rearrange("p (b j) -> p j b", j=SQUARE),
             )
@@ -263,7 +263,6 @@ def tile_tiledlinear_kernel(tc, x, weight_words, weight_scales, bias, out):
                 nc.sync.dma_start(out=out_rows[m * P : (m + 1) * P, n_cols], in_=result[:, first:last])
 
         on_scalar = nc.scalar.copy
-        on_vector = nc.vector.tensor_copy
         every_pass = list(range(PASSES))
 
         warm_psum = psum.tile([P, BANK], F32, name="warm_psum", tag="bank%d" % BANKS[0])
@@ -277,32 +276,32 @@ def tile_tiledlinear_kernel(tc, x, weight_words, weight_scales, bias, out):
             for c in range(2):
                 multiply(m, c, passes)
 
-        repeat_bias()
         for m in range(3):
             turn(m, 0)
+            warm_up(1)
             lay(m, 0, on_scalar)
             quantise(m, 0)
-        warm_up(2)
         for c in range(2):
             for m in range(2):
                 multiply(m, c, [0])
         multiply(2, 0, [0])
-        turn_bias()
         for m in range(3):
             sort_words(m, 1)
+        repeat_bias()
         both(0, [1])
         both(1, [1])
         turn(0, 1)
         lay(0, 1, on_scalar)
         turn(1, 1)
-        lay(1, 1, on_vector)
+        lay(1, 1, on_scalar)
         turn(2, 1)
         lay(2, 1, on_scalar)
-        sort_bias()
         for m in range(3):
             quantise(m, 1)
         for s in range(2):
             sort_words(3, s)
+        turn_bias()
+        sort_bias()
         multiply(2, 0, [1])
         multiply(2, 1, [0, 1])
         for m in range(3):

@@ -32,6 +32,8 @@ HEAD_TURN_BANKS = {(0, 0): 0, (1, 0): 1, (2, 0): 2, (0, 1): 0, (1, 1): 1, (2, 1)
 BANKS = [6, 7, 3, 2, 4, 0, 1, 5]
 HEAD_TILES = 4
 
+LAST_PARTS = (BANK // 2, BANK // 4, BANK // 4)
+
 FLOPS = 2 * TOKENS * K * N
 
 
@@ -61,10 +63,10 @@ def tile_tiledlinear_kernel(tc, x, weight_words, weight_scales, bias, out):
             for g in range(PASSES)
         ]
         w_planes = [keep.tile([P, HALF], U8, name="w_planes%d" % h, align_bytes=64) for h in range(HALVES)]
-        bias_part = keep.tile([P, N // SQUARE], BF16, name="bias_part")
+        bias_part = keep.tile([P, N // SQUARE], BF16, name="bias_part", align_bytes=64)
+        bias_striped = keep.tile([P, SQUARE], F32, name="bias_striped", align_bytes=64)
         bias_repeated = stage.tile([P, N // 2], F32, name="bias_repeated", tag="square_sorted", align_bytes=64)
-        bias_turned = stage.tile([P, N // 2], F32, name="bias_turned", tag="square_turned", align_bytes=64)
-        bias_all = keep.tile([P, N], BF16, name="bias_all")
+        bias_all = keep.tile([P, N], BF16, name="bias_all", align_bytes=64)
         ident = keep.tile([P, P], F32, name="ident")
         warm = keep.tile([P, BANK], BF16, name="warm")
         dummy = keep.tile([P, 1], F32, name="dummy")
@@ -107,10 +109,10 @@ def tile_tiledlinear_kernel(tc, x, weight_words, weight_scales, bias, out):
         load_w(1, 0, HALF)
         for m in range(3):
             load_x_half(m, 1)
-        nc.sync.dma_start(
-            out=bias_part[:],
-            in_=bias.rearrange("(j c) -> j c", j=SQUARE).unsqueeze(0).to_broadcast([QUADRANTS, SQUARE, N // SQUARE]),
-        )
+        for q in range(QUADRANTS):
+            nc.sync.dma_start(
+                out=bias_part[SQUARE * q : SQUARE * (q + 1), :], in_=bias.rearrange("(j c) -> j c", j=SQUARE)
+            )
         load_w(2, 0, HALF)
         load_x(3)
         load_w(3, 0, HALF)
@@ -138,9 +140,9 @@ def tile_tiledlinear_kernel(tc, x, weight_words, weight_scales, bias, out):
         turned = {}
         grouped = {}
 
-        def sort_words(m, s):
+        def sort_words(m, s, copy):
             x_sorted[m, s] = stage.tile([P, 2, 2, P], F32, name="x_sorted%d" % s)
-            nc.vector.tensor_copy(
+            copy(
                 out=x_sorted[m, s][:],
                 in_=x_raw[m][:, s * 2 * K_PASS : (s + 1) * 2 * K_PASS]
                 .bitcast(F32)
@@ -214,29 +216,27 @@ def tile_tiledlinear_kernel(tc, x, weight_words, weight_scales, bias, out):
                 in_=square_grouped[m][:, 2 * s : 2 * s + 2, :, :].rearrange("p g t j -> p (g t j)"),
             )
 
+        def stripe_bias():
+            nc.vector.transpose(out=bias_striped[:], in_=bias_part[:].bitcast(F32))
+
         def repeat_bias():
             nc.vector.tensor_copy(
                 out=bias_repeated[:].rearrange("p (b i) -> p b i", i=SQUARE),
-                in_=bias_part[:].bitcast(F32).unsqueeze(2).to_broadcast([P, SQUARE, SQUARE]),
+                in_=bias_striped[:].unsqueeze(2).to_broadcast([P, SQUARE, SQUARE]),
             )
 
         def turn_bias():
-            nc.vector.transpose(out=bias_turned[:], in_=bias_repeated[:])
-
-        def sort_bias():
-            nc.vector.tensor_copy(
-                out=bias_all[:].bitcast(F32).rearrange("p (j b) -> p j b", j=SQUARE),
-                in_=bias_turned[:].rearrange("p (b j) -> p j b", j=SQUARE),
-            )
+            nc.vector.transpose(out=bias_all[:].bitcast(F32), in_=bias_repeated[:])
 
         sums = {}
 
-        def multiply(m, c, passes, parts=1):
+        def multiply(m, c, passes, parts=(BANK,)):
             h, col = divmod(c * BANK, HALF)
             if passes[0] == 0:
                 sums[m, c] = psum.tile([P, BANK], F32, name="sums", tag="bank%d" % next_bank())
-            for part in range(parts):
-                first, last = part * BANK // parts, (part + 1) * BANK // parts
+            last = 0
+            for width in parts:
+                first, last = last, last + width
                 for g in passes:
                     x_cols = slice(g * P, g * P + P)
                     nc.tensor.matmul_mx(
@@ -249,10 +249,11 @@ def tile_tiledlinear_kernel(tc, x, weight_words, weight_scales, bias, out):
                         stop=(g == PASSES - 1),
                     )
 
-        def finish(m, c, parts=1):
+        def finish(m, c, parts=(BANK,)):
             result = results.tile([P, BANK], F32, name="result")
-            for part in range(parts):
-                first, last = part * BANK // parts, (part + 1) * BANK // parts
+            last = 0
+            for width in parts:
+                first, last = last, last + width
                 n_cols = slice(c * BANK + first, c * BANK + last)
                 nc.vector.tensor_tensor(
                     out=result[:, first:last],
@@ -281,13 +282,12 @@ def tile_tiledlinear_kernel(tc, x, weight_words, weight_scales, bias, out):
             warm_up(1)
             lay(m, 0, on_scalar)
             quantise(m, 0)
-        for c in range(2):
-            for m in range(2):
+        for m in range(2):
+            for c in range(2):
                 multiply(m, c, [0])
         multiply(2, 0, [0])
         for m in range(3):
-            sort_words(m, 1)
-        repeat_bias()
+            sort_words(m, 1, nc.vector.tensor_copy)
         both(0, [1])
         both(1, [1])
         turn(0, 1)
@@ -299,9 +299,10 @@ def tile_tiledlinear_kernel(tc, x, weight_words, weight_scales, bias, out):
         for m in range(3):
             quantise(m, 1)
         for s in range(2):
-            sort_words(3, s)
+            sort_words(3, s, on_scalar)
+        stripe_bias()
+        repeat_bias()
         turn_bias()
-        sort_bias()
         multiply(2, 0, [1])
         multiply(2, 1, [0, 1])
         for m in range(3):
@@ -335,20 +336,22 @@ def tile_tiledlinear_kernel(tc, x, weight_words, weight_scales, bias, out):
 
         run(3, 0)
         run(3, 1)
-        prepare(sort_words, [4, 5])
+        for m in (4, 5):
+            for s in range(2):
+                sort_words(m, s, on_scalar)
         for g in every_pass:
             for m in range(2):
                 for c in (2, 3):
                     multiply(m, c, [g])
                     if g == PASSES - 1:
                         finish(m, c)
-        raise_tiles([4, 5])
         run(2, 2)
-        prepare(quantise, [4])
         run(2, 3)
         run(3, 2)
-        prepare(quantise, [5])
+        raise_tiles([4, 5])
+        prepare(quantise, [4])
         run(3, 3)
+        prepare(quantise, [5])
         prepare(sort_squares, [6, 7])
         for m in range(4, TOKEN_TILES):
             ahead = m + 2 if m + 2 < TOKEN_TILES else None
@@ -363,5 +366,5 @@ def tile_tiledlinear_kernel(tc, x, weight_words, weight_scales, bias, out):
                 prepare(lay_squares, [ahead])
             if m < TOKEN_TILES - 1:
                 run(m, 3)
-        multiply(7, CHUNKS - 1, every_pass, 2)
-        finish(7, CHUNKS - 1, 2)
+        multiply(7, CHUNKS - 1, every_pass, LAST_PARTS)
+        finish(7, CHUNKS - 1, LAST_PARTS)

from contextlib import ExitStack

import concourse.mybir as mybir
from concourse.masks import make_identity

F32 = mybir.dt.float32
BF16 = mybir.dt.bfloat16
I32 = mybir.dt.int32
U32 = mybir.dt.uint32
U8 = mybir.dt.uint8
FP8X4 = mybir.dt.float8_e4m3fn_x4

P = 128
PACK = 4
K_PASS = P * PACK
TOKENS = 1024
K = 2048
N = 2048
PASSES = K // K_PASS
TOKEN_TILES = TOKENS // P
BANK = 512
CHUNKS = N // BANK
HALF = N // 2
HALVES = N // HALF
WARM_MATMULS = 4

SQUARE = 32
QUADRANTS = P // SQUARE
PLAIN_TILES = 6

HEAD_TURN_BANKS = {(0, 0): 0, (1, 0): 1, (2, 0): 2, (0, 1): 0, (1, 1): 1, (2, 1): 5, (3, 0): 1, (3, 1): 5}
BANKS = [6, 7, 3, 2, 4, 0, 1, 5]
HEAD_TILES = 4

LAST_PARTS = (BANK // 2, BANK // 4, BANK // 4)

FLOPS = 2 * TOKENS * K * N


def tile_tiledlinear_kernel(tc, x, weight_words, weight_scales, bias, out):
    nc = tc.nc
    x_rows = x.flatten_outer_dims()
    out_rows = out.flatten_outer_dims()

    with ExitStack() as ctx:
        keep = ctx.enter_context(tc.tile_pool(name="keep", bufs=1))
        stage = ctx.enter_context(tc.tile_pool(name="stage", bufs=4))
        results = ctx.enter_context(tc.tile_pool(name="results", bufs=TOKEN_TILES * CHUNKS))
        psum = ctx.enter_context(tc.psum_pool(name="psum", bufs=1))
        ctx.enter_context(tc.manual_schedule())

        x_raw = [keep.tile([P, K], BF16, name="x_raw%d" % m) for m in range(PLAIN_TILES)]
        runs = (TOKEN_TILES - PLAIN_TILES) * QUADRANTS
        square_raw = keep.tile([P, runs, PASSES, P], BF16, name="square_raw")
        x_codes = [
            keep.tile([P, PASSES * P], U32, name="x_codes%d" % m, align_bytes=64) for m in range(TOKEN_TILES)
        ]
        x_planes = [
            keep.tile([P, PASSES * P], U8, name="x_planes%d" % m, align_bytes=64) for m in range(TOKEN_TILES)
        ]
        w_codes = [
            [keep.tile([P, HALF], U32, name="w_codes%d_%d" % (g, h), align_bytes=64) for h in range(HALVES)]
            for g in range(PASSES)
        ]
        w_planes = [keep.tile([P, HALF], U8, name="w_planes%d" % h, align_bytes=64) for h in range(HALVES)]
        bias_part = keep.tile([P, N // SQUARE], BF16, name="bias_part", align_bytes=64)
        bias_striped = keep.tile([P, SQUARE], F32, name="bias_striped", align_bytes=64)
        bias_repeated = stage.tile([P, N // 2], F32, name="bias_repeated", tag="square_sorted", align_bytes=64)
        bias_all = keep.tile([P, N], BF16, name="bias_all", align_bytes=64)
        ident = keep.tile([P, P], F32, name="ident")
        warm = keep.tile([P, BANK], BF16, name="warm")
        dummy = keep.tile([P, 1], F32, name="dummy")
        dummy_out = keep.tile([P, 1], F32, name="dummy_out")

        nc.vector.memset(warm[:].bitcast(I32), 0)
        nc.vector.memset(dummy[:], 0.0)
        nc.gpsimd.memset(w_planes[0][:].bitcast(I32), 0)
        nc.vector.memset(w_planes[1][:].bitcast(I32), 0)
        nc.scalar.copy(out=dummy_out[:], in_=dummy[:])
        make_identity(nc, ident[:])

        def load_x(m):
            nc.sync.dma_start(out=x_raw[m][:], in_=x_rows[m * P : (m + 1) * P, :])

        def load_w_planes(h):
            for quadrant in range(4):
                nc.sync.dma_start(
                    out=w_planes[h][32 * quadrant : 32 * quadrant + 16, :].bitcast(I32),
                    in_=weight_scales[:, 4 * quadrant : 4 * quadrant + 4, h * HALF : (h + 1) * HALF].bitcast(I32),
                )

        def load_w(g, first, last):
            h = first // HALF
            w_bytes = weight_words[g].rearrange("p n t -> p (n t)")
            nc.sync.dma_start(
                out=w_codes[g][h][:, first - h * HALF : last - h * HALF].bitcast(I32),
                in_=w_bytes[:, PACK * first : PACK * last].bitcast(I32),
            )

        def load_x_half(m, s):
            cols = slice(s * 2 * K_PASS, (s + 1) * 2 * K_PASS)
            nc.sync.dma_start(out=x_raw[m][:, cols], in_=x_rows[m * P : (m + 1) * P, cols])

        load_x_half(0, 0)
        load_w_planes(0)
        for m in (1, 2):
            load_x_half(m, 0)
        load_w(0, 0, HALF)
        load_w(1, 0, HALF)
        for m in range(3):
            load_x_half(m, 1)
        for q in range(QUADRANTS):
            nc.sync.dma_start(
                out=bias_part[SQUARE * q : SQUARE * (q + 1), :], in_=bias.rearrange("(j c) -> j c", j=SQUARE)
            )
        load_w(2, 0, HALF)
        load_x(3)
        load_w(3, 0, HALF)
        load_w_planes(1)
        for g in range(PASSES):
            load_w(g, HALF, N)
        for m in range(4, PLAIN_TILES):
            load_x(m)
        square_rows = x_rows[PLAIN_TILES * P : TOKENS, :]
        for g in range(PASSES):
            for q in (0, 2, 1, 3):
                first = g * K_PASS + q * P
                nc.sync.dma_start(
                    out=square_raw[SQUARE * q : SQUARE * (q + 1), :, g, :],
                    in_=square_rows[:, first : first + P].rearrange("(r j) c -> j r c", j=SQUARE),
                )

        taken = []

        def next_bank():
            taken.append(BANKS[len(taken) % len(BANKS)])
            return taken[-1]

        x_sorted = {}
        turned = {}
        grouped = {}

        def sort_words(m, s, copy):
            x_sorted[m, s] = stage.tile([P, 2, 2, P], F32, name="x_sorted%d" % s)
            copy(
                out=x_sorted[m, s][:],
                in_=x_raw[m][:, s * 2 * K_PASS : (s + 1) * 2 * K_PASS]
                .bitcast(F32)
                .rearrange("t (g p u) -> t g u p", g=2, u=2),
            )

        def turn(m, s):
            bank = HEAD_TURN_BANKS[m, s] if m < HEAD_TILES else next_bank()
            turned[m, s] = psum.tile([P, 2, 2, P], F32, name="turned", tag="bank%d" % bank)
            for j in range(2):
                for u in range(2):
                    if (m, s) not in x_sorted:
                        first = (2 * s + j) * 2 * P + u
                        words = x_raw[m][:].bitcast(F32)[:, first : first + 2 * P - u : 2]
                    else:
                        words = x_sorted[m, s][:, j, u, :]
                    nc.tensor.transpose(turned[m, s][:, j, u, :], words, ident[:])

        def lay(m, s, copy):
            grouped[m, s] = stage.tile([P, 2, P, PACK], BF16, name="grouped%d" % s, align_bytes=64)
            copy(
                out=grouped[m, s][:].bitcast(F32),
                in_=turned[m, s][:].rearrange("p j u t -> p j t u"),
            )

        def quantise(m, s):
            cols = slice(s * 2 * P, (s + 1) * 2 * P)
            nc.vector.quantize_mx(
                out=x_codes[m][:, cols].bitcast(FP8X4),
                scales=x_planes[m][:, cols],
                in_=grouped[m, s][:].rearrange("p g t j -> p (g t j)"),
            )

        square_sorted = {}
        square_turned = {}
        square_grouped = {}

        def sort_squares(m, s):
            first = (m - PLAIN_TILES) * QUADRANTS + 2 * s
            if s == 0:
                square_sorted[m] = stage.tile([P, 2, K_PASS], F32, name="square_sorted", align_bytes=64)
            nc.scalar.copy(
                out=square_sorted[m][:, s, :].rearrange("p (b u i) -> p b u i", u=2, i=SQUARE),
                in_=square_raw[:, first : first + 2, :, :]
                .rearrange("p r g c -> p (r g c)")
                .bitcast(F32)
                .rearrange("p (b i u) -> p b u i", u=2, i=SQUARE),
            )

        def turn_squares(m, s):
            if s == 0:
                square_turned[m] = stage.tile([P, 2, K_PASS], F32, name="square_turned", align_bytes=64)
            nc.vector.transpose(out=square_turned[m][:, s, :], in_=square_sorted[m][:, s, :])

        def lay_squares(m, s):
            if s == 0:
                square_grouped[m] = stage.tile([P, PASSES, P, PACK], BF16, name="square_grouped", align_bytes=64)
            words = square_turned[m][:].rearrange("p s (r g u j) -> p (s r) g u j", r=2, g=PASSES, u=2)
            grouped_words = square_grouped[m][:].rearrange("p g t j -> p g (t j)").bitcast(F32)
            for g in range(2 * s, 2 * s + 2):
                nc.scalar.copy(
                    out=grouped_words[:, g, :].rearrange("p (r j u) -> p r j u", r=QUADRANTS, u=2),
                    in_=words[:, :, g, :, :].rearrange("p r u j -> p r j u"),
                )

        def quantise_squares(m, s):
            cols = slice(s * 2 * P, (s + 1) * 2 * P)
            nc.vector.quantize_mx(
                out=x_codes[m][:, cols].bitcast(FP8X4),
                scales=x_planes[m][:, cols],
                in_=square_grouped[m][:, 2 * s : 2 * s + 2, :, :].rearrange("p g t j -> p (g t j)"),
            )

        def stripe_bias():
            nc.vector.transpose(out=bias_striped[:], in_=bias_part[:].bitcast(F32))

        def repeat_bias():
            nc.vector.tensor_copy(
                out=bias_repeated[:].rearrange("p (b i) -> p b i", i=SQUARE),
                in_=bias_striped[:].unsqueeze(2).to_broadcast([P, SQUARE, SQUARE]),
            )

        def turn_bias():
            nc.vector.transpose(out=bias_all[:].bitcast(F32), in_=bias_repeated[:])

        sums = {}

        def multiply(m, c, passes, parts=(BANK,)):
            h, col = divmod(c * BANK, HALF)
            if passes[0] == 0:
                sums[m, c] = psum.tile([P, BANK], F32, name="sums", tag="bank%d" % next_bank())
            last = 0
            for width in parts:
                first, last = last, last + width
                for g in passes:
                    x_cols = slice(g * P, g * P + P)
                    nc.tensor.matmul_mx(
                        out=sums[m, c][:, first:last],
                        lhsT=x_codes[m][:, x_cols].bitcast(FP8X4),
                        lhsT_scale=x_planes[m][:, x_cols],
                        rhs=w_codes[g][h][:, col + first : col + last].bitcast(FP8X4),
                        rhs_scale=w_planes[h][4 * g : P, col + first : col + last],
                        start=(g == 0),
                        stop=(g == PASSES - 1),
                    )

        def finish(m, c, parts=(BANK,)):
            result = results.tile([P, BANK], F32, name="result")
            last = 0
            for width in parts:
                first, last = last, last + width
                n_cols = slice(c * BANK + first, c * BANK + last)
                nc.vector.tensor_tensor(
                    out=result[:, first:last],
                    in0=sums[m, c][:, first:last],
                    in1=bias_all[:, n_cols],
                    op=mybir.AluOpType.add,
                )
                nc.sync.dma_start(out=out_rows[m * P : (m + 1) * P, n_cols], in_=result[:, first:last])

        on_scalar = nc.scalar.copy
        every_pass = list(range(PASSES))

        warm_psum = psum.tile([P, BANK], F32, name="warm_psum", tag="bank%d" % BANKS[0])

        def warm_up(matmuls):
            for i in range(matmuls):
                nc.tensor.matmul(warm_psum[:], lhsT=warm[:, 0:P], rhs=warm[:], start=True, stop=True)

        warm_up(WARM_MATMULS)
        def both(m, passes):
            for c in range(2):
                multiply(m, c, passes)

        for m in range(3):
            turn(m, 0)
            warm_up(1)
            lay(m, 0, on_scalar)
            quantise(m, 0)
        for m in range(2):
            for c in range(2):
                multiply(m, c, [0])
        multiply(2, 0, [0])
        for m in range(3):
            sort_words(m, 1, nc.vector.tensor_copy)
        both(0, [1])
        both(1, [1])
        turn(0, 1)
        lay(0, 1, on_scalar)
        turn(1, 1)
        lay(1, 1, on_scalar)
        turn(2, 1)
        lay(2, 1, on_scalar)
        for m in range(3):
            quantise(m, 1)
        for s in range(2):
            sort_words(3, s, on_scalar)
        stripe_bias()
        repeat_bias()
        turn_bias()
        multiply(2, 0, [1])
        multiply(2, 1, [0, 1])
        for m in range(3):
            both(m, [2])
        for s in range(2):
            turn(3, s)
            lay(3, s, on_scalar)
        both(0, [3])
        for s in range(2):
            quantise(3, s)
        both(1, [3])
        both(2, [3])
        for m in range(3):
            for c in range(2):
                finish(m, c)

        def run(m, c):
            multiply(m, c, every_pass)
            finish(m, c)

        def prepare(step, tiles):
            for m in tiles:
                for s in range(2):
                    step(m, s)

        def raise_tiles(tiles):
            for m in tiles:
                for s in range(2):
                    turn(m, s)
                    lay(m, s, on_scalar)

        run(3, 0)
        run(3, 1)
        for m in (4, 5):
            for s in range(2):
                sort_words(m, s, on_scalar)
        for g in every_pass:
            for m in range(2):
                for c in (2, 3):
                    multiply(m, c, [g])
                    if g == PASSES - 1:
                        finish(m, c)
        run(2, 2)
        run(2, 3)
        run(3, 2)
        raise_tiles([4, 5])
        prepare(quantise, [4])
        run(3, 3)
        prepare(quantise, [5])
        prepare(sort_squares, [6, 7])
        for m in range(4, TOKEN_TILES):
            ahead = m + 2 if m + 2 < TOKEN_TILES else None
            run(m, 0)
            if m + 1 in (6, 7):
                prepare(quantise_squares, [m + 1])
            run(m, 1)
            if ahead:
                prepare(turn_squares, [ahead])
            run(m, 2)
            if ahead:
                prepare(lay_squares, [ahead])
            if m < TOKEN_TILES - 1:
                run(m, 3)
        multiply(7, CHUNKS - 1, every_pass, LAST_PARTS)
        finish(7, CHUNKS - 1, LAST_PARTS)
